import numpy as np
import ml_dtypes


def mxq(x, axis, fmt="e4m3"):
    dtype, down = {"e4m3": (ml_dtypes.float8_e4m3fn, 7), "e5m2": (ml_dtypes.float8_e5m2, 14)}[fmt]
    v = np.moveaxis(np.asarray(x, np.float32).astype(ml_dtypes.bfloat16).astype(np.float64), axis, -1)
    blocks = v.reshape(v.shape[:-1] + (-1, 32))
    amax = np.abs(blocks).max(-1, keepdims=True)
    byte = np.maximum(np.where(amax > 0, np.frexp(amax)[1] - 1 + 127, 0) - down, 1)
    scale = np.exp2(byte - 127.0)
    codes = (blocks / scale).astype(np.float32).astype(dtype).astype(np.float64)
    return np.moveaxis((codes * scale).reshape(v.shape), -1, axis)


WIDE = False


def mx_kscale(k):
    if not WIDE:
        return np.ones(k)
    levels = np.array([10, -10, 5, -5, 0])
    a = np.random.permutation(np.resize(levels, k // 512 * 4)).reshape(k // 512, 4)
    idx = np.arange(k)
    return np.exp2(a[idx // 512, idx % 128 // 32])


BF16 = ml_dtypes.bfloat16


def bf(x):
    return np.asarray(x, np.float32).astype(BF16)


def f64(x):
    return np.asarray(x).astype(np.float64)


N, C0, C1, C2, C, R0, R1, R2, R3, R4, NQ, F, NCW = 8, 64, 128, 256, 8192, 128, 128, 64, 8, 4, 512, 512, 128
GRAD_BOOST = 10.0
EPS = 1e-8


def norm_rows(v):
    return (v - v.mean(-1, keepdims=True)) / (v.std(-1, ddof=1, keepdims=True) + EPS)


def quad(x, w):
    n, c, h, wd = x.shape
    mt = x.reshape(n, c, h * wd).transpose(0, 2, 1)
    z = w * GRAD_BOOST
    e = np.exp(z - z.max(0, keepdims=True))
    sm = e / e.sum(0, keepdims=True)
    proj = mxq(mt, 2, "e4m3") @ mxq(sm, 0, "e4m3")
    return (proj ** 2).sum(1)


def draw_x(r, s):
    g = np.exp(0.7 * np.random.standard_normal((N, C, 1, 1)))
    return bf(np.random.standard_normal((N, C, r, r)) * g / s[None, :, None, None])


def draw_w(s):
    return bf(0.5 * np.random.uniform(size=(C, NQ)) + np.log(s)[:, None] / GRAD_BOOST)


def setup_inputs():
    s3, s4 = mx_kscale(C), mx_kscale(C)
    return {"x3": draw_x(R3, s3), "x4": draw_x(R4, s4), "w1_3": draw_w(s3), "w1_4": draw_w(s4)}


def reference(x3, x4, w1_3, w1_4):
    f3 = norm_rows(quad(f64(x3), f64(w1_3)))
    f4 = norm_rows(quad(f64(x4), f64(w1_4)))
    return np.concatenate([f3, f4], axis=1)

@@ -1,0 +1,320 @@
+from contextlib import ExitStack
+
+import concourse.mybir as mybir
+from concourse.masks import make_identity
+
+F32 = mybir.dt.float32
+BF16 = mybir.dt.bfloat16
+U32 = mybir.dt.uint32
+U8 = mybir.dt.uint8
+FP8X4 = mybir.dt.float8_e4m3fn_x4
+ALU = mybir.AluOpType
+ACT = mybir.ActivationFunctionType
+AXIS_X = mybir.AxisListType.X
+
+P = 128
+PACK = 4
+K_PASS = P * PACK
+CHANNELS = 8192
+PASSES = CHANNELS // K_PASS
+SAMPLES = 8
+COLUMNS = 512
+LANES = 2
+GROUP_COLUMNS = P * LANES
+GROUPS = COLUMNS // GROUP_COLUMNS
+CHUNK_PASSES = 4
+CHUNKS = PASSES // CHUNK_PASSES
+CHUNK_CHANNELS = CHUNK_PASSES * K_PASS
+QUANT_WIDTH = 2048
+GRAD_BOOST = 10.0
+EPS = 1e-8
+
+FLOPS = 2 * SAMPLES * (64 + 16) * CHANNELS * COLUMNS
+
+
+def quantise_x_tile(nc, stage, x, positions, codes, scales, first):
+    passes = QUANT_WIDTH // (PACK * SAMPLES * positions)
+    raw = stage.tile([P, passes, SAMPLES, PACK * positions], BF16, name="x_raw")
+    for i in range(passes):
+        rows = slice((first + i) * K_PASS, (first + i + 1) * K_PASS)
+        nc.sync.dma_start(
+            out=raw[:, i], in_=x[:, rows].rearrange("n (q j) h w -> q n (j h w)", j=PACK)
+        )
+    grouped = stage.tile([P, passes * SAMPLES, positions, PACK], BF16, name="x_grouped", align_bytes=64)
+    nc.vector.tensor_copy(out=grouped[:], in_=raw[:].rearrange("q c n (j f) -> q (c n) f j", j=PACK))
+    these = slice(first, first + passes)
+    nc.vector.quantize_mx(
+        out=codes[:, these, :].rearrange("q c m -> q (c m)").bitcast(FP8X4),
+        scales=scales[:, these, :].rearrange("q c m -> q (c m)"),
+        in_=grouped[:].rearrange("q a f j -> q (a f j)"),
+    )
+
+
+def group_statistics(pools):
+    chunk_max = pools["stats"].tile([P, LANES, CHUNKS], F32, name="chunk_max")
+    shift = pools["stats"].tile([P, LANES, CHUNKS], F32, name="shift")
+    sums = pools["stats"].tile([P, LANES, CHUNKS, CHUNK_PASSES], F32, name="sums")
+    return chunk_max, shift, sums
+
+
+def exponentials(nc, pools, ident, w, group, chunk, statistics):
+    chunk_max, shift, sums = statistics
+    columns = slice(group * GROUP_COLUMNS, (group + 1) * GROUP_COLUMNS)
+    w_chunk = pools["w"].tile([P, CHUNK_PASSES, PACK, GROUP_COLUMNS], BF16, name="w_chunk")
+    for l in range(CHUNK_PASSES):
+        first_row = (chunk * CHUNK_PASSES + l) * K_PASS
+        nc.sync.dma_start(
+            out=w_chunk[:, l],
+            in_=w[first_row : first_row + K_PASS, columns].rearrange("(q j) o -> q j o", j=PACK),
+        )
+
+    best = pools["best"].tile([P, 8 * GROUP_COLUMNS], BF16, name="best")
+    nc.vector.tensor_tensor(
+        out=best[:],
+        in0=w_chunk[:, 0:2].rearrange("q l j o -> q (l j o)"),
+        in1=w_chunk[:, 2:4].rearrange("q l j o -> q (l j o)"),
+        op=ALU.max,
+    )
+    for rows in (4, 2, 1):
+        half = rows * GROUP_COLUMNS
+        nc.vector.tensor_tensor(
+            out=best[:, 0:half], in0=best[:, 0:half], in1=best[:, half : 2 * half], op=ALU.max
+        )
+    best_t = pools["psum_small"].tile([P, P], F32, name="best_t", tag="small")
+    nc.tensor.transpose(best_t[:], best[:, 0:GROUP_COLUMNS].bitcast(F32), ident[:])
+    nc.vector.tensor_reduce(
+        out=chunk_max[:, :, chunk],
+        in_=best_t[:].bitcast(BF16).rearrange("i (q e) -> i e q", e=LANES),
+        axis=AXIS_X,
+        op=ALU.max,
+    )
+    nc.vector.tensor_scalar(
+        out=shift[:, :, chunk],
+        in0=chunk_max[:, :, chunk],
+        scalar1=-GRAD_BOOST,
+        scalar2=None,
+        op0=ALU.mult,
+    )
+
+    lanes = [
+        pools["e"].tile([P, CHUNK_CHANNELS], F32, name="e_lane%d" % lane, tag="e_tile")
+        for lane in range(LANES)
+    ]
+    w_words = w_chunk[:].bitcast(F32)
+    for l in range(CHUNK_PASSES):
+        w_t = pools["psum_w"].tile([P, PACK, P], F32, name="w_t")
+        for j in range(PACK):
+            nc.tensor.transpose(w_t[:, j, :], w_words[:, l, j, :], ident[:])
+        by_lane = w_t[:].bitcast(BF16).rearrange("i (u k) (q e) -> i e u q k", k=2, e=LANES)
+        for lane in range(LANES):
+            nc.scalar.activation(
+                out=lanes[lane][:, l * K_PASS : (l + 1) * K_PASS].rearrange(
+                    "i (u q k) -> i u q k", u=2, k=2
+                ),
+                in_=by_lane[:, lane],
+                func=ACT.Exp,
+                bias=shift[:, lane, chunk : chunk + 1],
+                scale=GRAD_BOOST,
+                accum_out=sums[:, lane, chunk, l : l + 1],
+            )
+    return lanes
+
+
+def column_gain(nc, pools, statistics):
+    chunk_max, sums = statistics[0], statistics[2]
+    stats = pools["stats"]
+    shape = [P, LANES, CHUNKS]
+
+    col_max = stats.tile([P, LANES], F32, name="col_max")
+    nc.vector.tensor_reduce(out=col_max[:], in_=chunk_max[:], axis=AXIS_X, op=ALU.max)
+    below = stats.tile(shape, F32, name="below")
+    nc.vector.tensor_tensor(
+        out=below[:], in0=chunk_max[:], in1=col_max[:].unsqueeze(2).to_broadcast(shape), op=ALU.subtract
+    )
+    rescale = stats.tile(shape, F32, name="rescale")
+    nc.scalar.activation(out=rescale[:], in_=below[:], func=ACT.Exp, scale=GRAD_BOOST)
+    chunk_sum = stats.tile(shape, F32, name="chunk_sum")
+    nc.vector.tensor_reduce(out=chunk_sum[:], in_=sums[:], axis=AXIS_X, op=ALU.add)
+    nc.vector.tensor_tensor(out=chunk_sum[:], in0=chunk_sum[:], in1=rescale[:], op=ALU.mult)
+    col_sum = stats.tile([P, LANES], F32, name="col_sum")
+    nc.vector.tensor_reduce(out=col_sum[:], in_=chunk_sum[:], axis=AXIS_X, op=ALU.add)
+    nc.vector.reciprocal(out=col_sum[:], in_=col_sum[:])
+    gain = stats.tile(shape, F32, name="gain")
+    nc.vector.tensor_tensor(
+        out=gain[:], in0=rescale[:], in1=col_sum[:].unsqueeze(2).to_broadcast(shape), op=ALU.mult
+    )
+    return gain
+
+
+def project(nc, pools, ident, e_lanes, gain, chunk, proj, x_codes, x_scales, width):
+    for lane in range(LANES):
+        sm_t = pools["sm"].tile([P, CHUNK_CHANNELS], BF16, name="sm_t")
+        nc.vector.tensor_scalar(
+            out=sm_t[:],
+            in0=e_lanes[lane][:],
+            scalar1=gain[:, lane, chunk : chunk + 1],
+            scalar2=None,
+            op0=ALU.mult,
+        )
+        sm_words = sm_t[:].bitcast(F32)
+        grouped = pools["sm"].tile([P, CHUNK_PASSES, P, PACK], BF16, name="sm_grouped", align_bytes=64)
+        grouped_words = grouped[:].bitcast(F32)
+        for pair in range(CHUNK_PASSES // 2):
+            back = pools["psum_back"].tile([P, 4, P], F32, name="back")
+            for r in range(4):
+                run = (4 * pair + r) * P
+                nc.tensor.transpose(back[:, r, :], sm_words[:, run : run + P], ident[:])
+            nc.scalar.copy(
+                out=grouped_words[:, 2 * pair : 2 * pair + 2],
+                in_=back[:].rearrange("q (l u) i -> q l i u", u=2),
+            )
+        sm_codes = pools["codes"].tile([P, CHUNK_PASSES * P], U32, name="sm_codes", align_bytes=64)
+        sm_scales = pools["codes"].tile([P, CHUNK_PASSES * P], U8, name="sm_scales", align_bytes=64)
+        nc.vector.quantize_mx(
+            out=sm_codes[:].bitcast(FP8X4),
+            scales=sm_scales[:],
+            in_=grouped[:].rearrange("q l i t -> q (l i t)"),
+        )
+        for l in range(CHUNK_PASSES):
+            c = chunk * CHUNK_PASSES + l
+            nc.tensor.matmul_mx(
+                out=proj[lane][:, 0:width],
+                lhsT=sm_codes[:, l * P : (l + 1) * P].bitcast(FP8X4),
+                lhsT_scale=sm_scales[:, l * P : (l + 1) * P],
+                rhs=x_codes[:, c, :].bitcast(FP8X4),
+                rhs_scale=x_scales[:, c, :],
+                start=(c == 0),
+                stop=(c == PASSES - 1),
+            )
+
+
+def sum_squares(nc, pools, proj, width, q_t, first_slot, first_col):
+    for lane in range(LANES):
+        squares = pools["row"].tile([P, COLUMNS], F32, name="squares", tag="row")
+        nc.scalar.activation(out=squares[:, 0:width], in_=proj[lane][:, 0:width], func=ACT.Square)
+        nc.vector.tensor_reduce(
+            out=q_t[:, first_slot + lane, first_col : first_col + SAMPLES],
+            in_=squares[:, 0:width].rearrange("i (n f) -> i n f", n=SAMPLES),
+            axis=AXIS_X,
+            op=ALU.add,
+        )
+
+
+def normalise_rows(nc, pools, ident, q_t, out):
+    rows = 2 * SAMPLES
+    q_rows = pools["psum_small"].tile([P, 2 * GROUPS, P], F32, name="q_rows", tag="small")
+    for slot in range(2 * GROUPS):
+        nc.tensor.transpose(q_rows[:, slot, :], q_t[:, slot, :], ident[:])
+    stats = pools["stats"]
+    mean = stats.tile([P, 1], F32, name="mean")
+    nc.vector.tensor_reduce(
+        out=mean[0:rows], in_=q_rows[0:rows].rearrange("r s i -> r (s i)"), axis=AXIS_X, op=ALU.add
+    )
+    nc.vector.tensor_scalar(
+        out=mean[0:rows], in0=mean[0:rows], scalar1=1.0 / COLUMNS, scalar2=None, op0=ALU.mult
+    )
+    centred = pools["row"].tile([P, COLUMNS], F32, name="centred", tag="row")
+    nc.vector.tensor_scalar(
+        out=centred[0:rows].rearrange("r (g i e) -> r g i e", g=GROUPS, e=LANES),
+        in0=q_rows[0:rows].rearrange("r (g e) i -> r g i e", e=LANES),
+        scalar1=mean[0:rows, 0:1],
+        scalar2=None,
+        op0=ALU.subtract,
+    )
+    squares = pools["row"].tile([P, COLUMNS], F32, name="dev_squares", tag="row")
+    spread = stats.tile([P, 1], F32, name="spread")
+    nc.scalar.activation(
+        out=squares[0:rows], in_=centred[0:rows], func=ACT.Square, accum_out=spread[0:rows, 0:1]
+    )
+    std = stats.tile([P, 1], F32, name="std")
+    nc.scalar.activation(
+        out=std[0:rows], in_=spread[0:rows], func=ACT.Sqrt, scale=1.0 / (COLUMNS - 1)
+    )
+    inverse = stats.tile([P, 1], F32, name="inverse")
+    nc.vector.tensor_scalar(
+        out=inverse[0:rows], in0=std[0:rows], scalar1=EPS, scalar2=None, op0=ALU.add
+    )
+    nc.vector.reciprocal(out=inverse[0:rows], in_=inverse[0:rows])
+    result = pools["row"].tile([P, COLUMNS], F32, name="result", tag="row")
+    nc.vector.tensor_scalar(
+        out=result[0:rows],
+        in0=centred[0:rows],
+        scalar1=inverse[0:rows, 0:1],
+        scalar2=None,
+        op0=ALU.mult,
+    )
+    for s in range(2):
+        nc.sync.dma_start(
+            out=out[:, s * COLUMNS : (s + 1) * COLUMNS], in_=result[s * SAMPLES : (s + 1) * SAMPLES]
+        )
+
+
+def tile_texture_encoder_pa_k_kernel(tc, x3, x4, w1_3, w1_4, out):
+    nc = tc.nc
+    with ExitStack() as ctx:
+        pools = {
+            "const": ctx.enter_context(tc.tile_pool(name="const", bufs=1)),
+            "x_keep": ctx.enter_context(tc.tile_pool(name="x_keep", bufs=1)),
+            "x_stage": ctx.enter_context(tc.tile_pool(name="x_stage", bufs=2)),
+            "w": ctx.enter_context(tc.tile_pool(name="w", bufs=4)),
+            "best": ctx.enter_context(tc.tile_pool(name="best", bufs=2)),
+            "e": ctx.enter_context(tc.tile_pool(name="e", bufs=LANES * CHUNKS + LANES)),
+            "sm": ctx.enter_context(tc.tile_pool(name="sm", bufs=2)),
+            "codes": ctx.enter_context(tc.tile_pool(name="codes", bufs=4)),
+            "row": ctx.enter_context(tc.tile_pool(name="row", bufs=3)),
+            "stats": ctx.enter_context(tc.tile_pool(name="stats", bufs=2)),
+            "psum_w": ctx.enter_context(tc.psum_pool(name="psum_w", bufs=3)),
+            "psum_back": ctx.enter_context(tc.psum_pool(name="psum_back", bufs=2)),
+            "psum_proj": ctx.enter_context(tc.psum_pool(name="psum_proj", bufs=2)),
+            "psum_small": ctx.enter_context(tc.psum_pool(name="psum_small", bufs=1)),
+        }
+        ident = pools["const"].tile([P, P], F32, name="ident")
+        make_identity(nc, ident[:])
+        q_t = pools["const"].tile([P, 2 * GROUPS, P], F32, name="q_t")
+        nc.vector.memset(q_t[:], 0.0)
+
+        x4_codes = pools["x_keep"].tile([P, PASSES, SAMPLES * 16], U32, name="x4_codes", align_bytes=64)
+        x4_scales = pools["x_keep"].tile([P, PASSES, SAMPLES * 16], U8, name="x4_scales", align_bytes=64)
+        x3_codes = pools["x_keep"].tile([P, PASSES, SAMPLES * 64], U32, name="x3_codes", align_bytes=64)
+        x3_scales = pools["x_keep"].tile([P, PASSES, SAMPLES * 64], U8, name="x3_scales", align_bytes=64)
+
+        jobs = []
+        for group in range(GROUPS):
+            jobs.append((w1_4, group, x4_codes, x4_scales, 16, SAMPLES))
+        for group in range(GROUPS):
+            jobs.append((w1_3, group, x3_codes, x3_scales, 64, 0))
+
+        statistics = group_statistics(pools)
+        e_tiles = [
+            exponentials(nc, pools, ident, jobs[0][0], jobs[0][1], chunk, statistics)
+            for chunk in range(CHUNKS)
+        ]
+        for first in range(0, PASSES, 4):
+            quantise_x_tile(nc, pools["x_stage"], x4, 16, x4_codes, x4_scales, first)
+        for index in range(len(jobs)):
+            group, x_codes, x_scales, positions, first_col = jobs[index][1:]
+            width = SAMPLES * positions
+            more = index + 1 < len(jobs)
+            next_tiles = []
+            if more:
+                next_w, next_group = jobs[index + 1][0], jobs[index + 1][1]
+                next_statistics = group_statistics(pools)
+                next_tiles.append(exponentials(nc, pools, ident, next_w, next_group, 0, next_statistics))
+            gain = column_gain(nc, pools, statistics)
+            proj = [
+                pools["psum_proj"].tile([P, COLUMNS], F32, name="proj%d" % lane, tag="proj")
+                for lane in range(LANES)
+            ]
+            for chunk in range(CHUNKS):
+                project(nc, pools, ident, e_tiles[chunk], gain, chunk, proj, x_codes, x_scales, width)
+                if index < GROUPS:
+                    for first in range(2 * (index * CHUNKS + chunk), 2 * (index * CHUNKS + chunk) + 2):
+                        quantise_x_tile(nc, pools["x_stage"], x3, 64, x3_codes, x3_scales, first)
+                if more and chunk + 1 < CHUNKS:
+                    next_tiles.append(
+                        exponentials(nc, pools, ident, next_w, next_group, chunk + 1, next_statistics)
+                    )
+            sum_squares(nc, pools, proj, width, q_t, LANES * group, first_col)
+            if more:
+                statistics, e_tiles = next_statistics, next_tiles
+        normalise_rows(nc, pools, ident, q_t, out)

@@ -26,27 +26,43 @@ CHUNK_PASSES = 4
 CHUNKS = PASSES // CHUNK_PASSES
 CHUNK_CHANNELS = CHUNK_PASSES * K_PASS
 QUANT_WIDTH = 2048
+W_AHEAD = 3
+STAGE2_LAG = CHUNKS
+STAGE3_LAG = STAGE2_LAG + 1
+X4_FIRST_STEP = 2
 GRAD_BOOST = 10.0
 EPS = 1e-8
 
 FLOPS = 2 * SAMPLES * (64 + 16) * CHANNELS * COLUMNS
 
 
-def quantise_x_tile(nc, stage, x, positions, codes, scales, first):
+def load_x_tile(nc, pools, x, positions, first):
     passes = QUANT_WIDTH // (PACK * SAMPLES * positions)
-    raw = stage.tile([P, passes, SAMPLES, PACK * positions], BF16, name="x_raw")
+    raw = pools["x_raw"].tile([P, passes, SAMPLES, PACK * positions], BF16, name="x_raw")
     for i in range(passes):
         rows = slice((first + i) * K_PASS, (first + i + 1) * K_PASS)
         nc.sync.dma_start(
-            out=raw[:, i], in_=x[:, rows].rearrange("n (q j) h w -> q n (j h w)", j=PACK)
+            out=raw[:, i], in_=x[:, rows].rearrange("n (q t) h w -> q n (t h w)", t=PACK)
         )
-    grouped = stage.tile([P, passes * SAMPLES, positions, PACK], BF16, name="x_grouped", align_bytes=64)
-    nc.vector.tensor_copy(out=grouped[:], in_=raw[:].rearrange("q c n (j f) -> q (c n) f j", j=PACK))
-    these = slice(first, first + passes)
+    return raw
+
+
+def regroup_x_tile(nc, pools, raw, positions):
+    grouped = pools["x_grouped"].tile([P, QUANT_WIDTH // (PACK * positions), positions, PACK], BF16,
+                                      name="x_grouped", align_bytes=64)
+    nc.vector.tensor_copy(
+        out=grouped[:].rearrange("q a (c i) t -> q a c t i", i=4),
+        in_=raw[:].rearrange("q l n (t c i) -> q (l n) c t i", t=PACK, i=4),
+    )
+    return grouped
+
+
+def quantise_x_tile(nc, grouped, codes, scales, first, positions):
+    these = slice(first, first + QUANT_WIDTH // (PACK * SAMPLES * positions))
     nc.vector.quantize_mx(
         out=codes[:, these, :].rearrange("q c m -> q (c m)").bitcast(FP8X4),
         scales=scales[:, these, :].rearrange("q c m -> q (c m)"),
-        in_=grouped[:].rearrange("q a f j -> q (a f j)"),
+        in_=grouped[:].rearrange("q a f t -> q (a f t)"),
     )
 
 
@@ -57,22 +73,25 @@ def group_statistics(pools):
     return chunk_max, shift, sums
 
 
-def exponentials(nc, pools, ident, w, group, chunk, statistics):
-    chunk_max, shift, sums = statistics
+def load_w_chunk(nc, pools, w, group, chunk):
     columns = slice(group * GROUP_COLUMNS, (group + 1) * GROUP_COLUMNS)
     w_chunk = pools["w"].tile([P, CHUNK_PASSES, PACK, GROUP_COLUMNS], BF16, name="w_chunk")
     for l in range(CHUNK_PASSES):
         first_row = (chunk * CHUNK_PASSES + l) * K_PASS
         nc.sync.dma_start(
             out=w_chunk[:, l],
-            in_=w[first_row : first_row + K_PASS, columns].rearrange("(q j) o -> q j o", j=PACK),
+            in_=w[first_row : first_row + K_PASS, columns].rearrange("(q t) o -> q t o", t=PACK),
         )
+    return w_chunk
 
+
+def chunk_maxima(nc, pools, ident, w_chunk, statistics, chunk):
+    chunk_max, shift = statistics[0], statistics[1]
     best = pools["best"].tile([P, 8 * GROUP_COLUMNS], BF16, name="best")
     nc.vector.tensor_tensor(
         out=best[:],
-        in0=w_chunk[:, 0:2].rearrange("q l j o -> q (l j o)"),
-        in1=w_chunk[:, 2:4].rearrange("q l j o -> q (l j o)"),
+        in0=w_chunk[:, 0:2].rearrange("q l t o -> q (l t o)"),
+        in1=w_chunk[:, 2:4].rearrange("q l t o -> q (l t o)"),
         op=ALU.max,
     )
     for rows in (4, 2, 1):
@@ -96,96 +115,108 @@ def exponentials(nc, pools, ident, w, group, chunk, statistics):
         op0=ALU.mult,
     )
 
-    lanes = [
-        pools["e"].tile([P, CHUNK_CHANNELS], F32, name="e_lane%d" % lane, tag="e_tile")
-        for lane in range(LANES)
-    ]
+
+def transpose_pass(nc, pools, ident, w_chunk, l):
     w_words = w_chunk[:].bitcast(F32)
-    for l in range(CHUNK_PASSES):
-        w_t = pools["psum_w"].tile([P, PACK, P], F32, name="w_t")
-        for j in range(PACK):
-            nc.tensor.transpose(w_t[:, j, :], w_words[:, l, j, :], ident[:])
-        by_lane = w_t[:].bitcast(BF16).rearrange("i (u k) (q e) -> i e u q k", k=2, e=LANES)
-        for lane in range(LANES):
-            nc.scalar.activation(
-                out=lanes[lane][:, l * K_PASS : (l + 1) * K_PASS].rearrange(
-                    "i (u q k) -> i u q k", u=2, k=2
-                ),
-                in_=by_lane[:, lane],
-                func=ACT.Exp,
-                bias=shift[:, lane, chunk : chunk + 1],
-                scale=GRAD_BOOST,
-                accum_out=sums[:, lane, chunk, l : l + 1],
-            )
-    return lanes
+    w_t = pools["psum_w"].tile([P, PACK, P], F32, name="w_t")
+    for t in range(PACK):
+        nc.tensor.transpose(w_t[:, t, :], w_words[:, l, t, :], ident[:])
+    return w_t
 
 
-def column_gain(nc, pools, statistics):
-    chunk_max, sums = statistics[0], statistics[2]
-    stats = pools["stats"]
+def exponentials(nc, w_t, e_lanes, statistics, chunk, l):
+    shift, sums = statistics[1], statistics[2]
+    by_lane = w_t[:].bitcast(BF16).rearrange("i (u k) (q e) -> i e u q k", k=2, e=LANES)
+    for lane in range(LANES):
+        nc.scalar.activation(
+            out=e_lanes[lane][:, l * K_PASS : (l + 1) * K_PASS].rearrange(
+                "i (u q k) -> i u q k", u=2, k=2
+            ),
+            in_=by_lane[:, lane],
+            func=ACT.Exp,
+            bias=shift[:, lane, chunk : chunk + 1],
+            scale=GRAD_BOOST,
+            accum_out=sums[:, lane, chunk, l : l + 1],
+        )
+
+
+def chunk_rescale(nc, pools, statistics):
+    chunk_max = statistics[0]
     shape = [P, LANES, CHUNKS]
-
-    col_max = stats.tile([P, LANES], F32, name="col_max")
+    col_max = pools["stats"].tile([P, LANES], F32, name="col_max")
     nc.vector.tensor_reduce(out=col_max[:], in_=chunk_max[:], axis=AXIS_X, op=ALU.max)
-    below = stats.tile(shape, F32, name="below")
+    below = pools["stats"].tile(shape, F32, name="below")
     nc.vector.tensor_tensor(
         out=below[:], in0=chunk_max[:], in1=col_max[:].unsqueeze(2).to_broadcast(shape), op=ALU.subtract
     )
-    rescale = stats.tile(shape, F32, name="rescale")
+    rescale = pools["stats"].tile(shape, F32, name="rescale")
     nc.scalar.activation(out=rescale[:], in_=below[:], func=ACT.Exp, scale=GRAD_BOOST)
-    chunk_sum = stats.tile(shape, F32, name="chunk_sum")
+    return rescale
+
+
+def column_gain(nc, pools, statistics, rescale):
+    sums = statistics[2]
+    shape = [P, LANES, CHUNKS]
+    chunk_sum = pools["stats"].tile(shape, F32, name="chunk_sum")
     nc.vector.tensor_reduce(out=chunk_sum[:], in_=sums[:], axis=AXIS_X, op=ALU.add)
     nc.vector.tensor_tensor(out=chunk_sum[:], in0=chunk_sum[:], in1=rescale[:], op=ALU.mult)
-    col_sum = stats.tile([P, LANES], F32, name="col_sum")
+    col_sum = pools["stats"].tile([P, LANES], F32, name="col_sum")
     nc.vector.tensor_reduce(out=col_sum[:], in_=chunk_sum[:], axis=AXIS_X, op=ALU.add)
     nc.vector.reciprocal(out=col_sum[:], in_=col_sum[:])
-    gain = stats.tile(shape, F32, name="gain")
+    gain = pools["stats"].tile(shape, F32, name="gain")
     nc.vector.tensor_tensor(
         out=gain[:], in0=rescale[:], in1=col_sum[:].unsqueeze(2).to_broadcast(shape), op=ALU.mult
     )
     return gain
 
 
-def project(nc, pools, ident, e_lanes, gain, chunk, proj, x_codes, x_scales, width):
-    for lane in range(LANES):
-        sm_t = pools["sm"].tile([P, CHUNK_CHANNELS], BF16, name="sm_t")
-        nc.vector.tensor_scalar(
-            out=sm_t[:],
-            in0=e_lanes[lane][:],
-            scalar1=gain[:, lane, chunk : chunk + 1],
-            scalar2=None,
-            op0=ALU.mult,
+def normalise(nc, pools, e_lane, gain_column):
+    sm_t = pools["sm_t"].tile([P, CHUNK_CHANNELS], BF16, name="sm_t")
+    nc.vector.tensor_scalar(
+        out=sm_t[:], in0=e_lane[:], scalar1=gain_column, scalar2=None, op0=ALU.mult
+    )
+    return sm_t
+
+
+def transpose_back(nc, pools, ident, sm_t):
+    sm_words = sm_t[:].bitcast(F32)
+    grouped = pools["sm_grouped"].tile([P, CHUNK_PASSES, P, PACK], BF16, name="sm_grouped", align_bytes=64)
+    grouped_words = grouped[:].bitcast(F32)
+    for pair in range(CHUNK_PASSES // 2):
+        back = pools["psum_back"].tile([P, 4, P], F32, name="back")
+        for r in range(4):
+            run = (4 * pair + r) * P
+            nc.tensor.transpose(back[:, r, :], sm_words[:, run : run + P], ident[:])
+        nc.scalar.copy(
+            out=grouped_words[:, 2 * pair : 2 * pair + 2],
+            in_=back[:].rearrange("q (l u) i -> q l i u", u=2),
         )
-        sm_words = sm_t[:].bitcast(F32)
-        grouped = pools["sm"].tile([P, CHUNK_PASSES, P, PACK], BF16, name="sm_grouped", align_bytes=64)
-        grouped_words = grouped[:].bitcast(F32)
-        for pair in range(CHUNK_PASSES // 2):
-            back = pools["psum_back"].tile([P, 4, P], F32, name="back")
-            for r in range(4):
-                run = (4 * pair + r) * P
-                nc.tensor.transpose(back[:, r, :], sm_words[:, run : run + P], ident[:])
-            nc.scalar.copy(
-                out=grouped_words[:, 2 * pair : 2 * pair + 2],
-                in_=back[:].rearrange("q (l u) i -> q l i u", u=2),
-            )
-        sm_codes = pools["codes"].tile([P, CHUNK_PASSES * P], U32, name="sm_codes", align_bytes=64)
-        sm_scales = pools["codes"].tile([P, CHUNK_PASSES * P], U8, name="sm_scales", align_bytes=64)
-        nc.vector.quantize_mx(
-            out=sm_codes[:].bitcast(FP8X4),
-            scales=sm_scales[:],
-            in_=grouped[:].rearrange("q l i t -> q (l i t)"),
+    return grouped
+
+
+def quantise_sm(nc, pools, grouped):
+    sm_codes = pools["codes"].tile([P, CHUNK_PASSES * P], U32, name="sm_codes", align_bytes=64)
+    sm_scales = pools["codes"].tile([P, CHUNK_PASSES * P], U8, name="sm_scales", align_bytes=64)
+    nc.vector.quantize_mx(
+        out=sm_codes[:].bitcast(FP8X4),
+        scales=sm_scales[:],
+        in_=grouped[:].rearrange("q l i t -> q (l i t)"),
+    )
+    return sm_codes, sm_scales
+
+
+def multiply(nc, proj_lane, sm_codes, sm_scales, x_codes, x_scales, chunk):
+    for l in range(CHUNK_PASSES):
+        c = chunk * CHUNK_PASSES + l
+        nc.tensor.matmul_mx(
+            out=proj_lane,
+            lhsT=sm_codes[:, l * P : (l + 1) * P].bitcast(FP8X4),
+            lhsT_scale=sm_scales[:, l * P : (l + 1) * P],
+            rhs=x_codes[:, c, :].bitcast(FP8X4),
+            rhs_scale=x_scales[:, c, :],
+            start=(c == 0),
+            stop=(c == PASSES - 1),
         )
-        for l in range(CHUNK_PASSES):
-            c = chunk * CHUNK_PASSES + l
-            nc.tensor.matmul_mx(
-                out=proj[lane][:, 0:width],
-                lhsT=sm_codes[:, l * P : (l + 1) * P].bitcast(FP8X4),
-                lhsT_scale=sm_scales[:, l * P : (l + 1) * P],
-                rhs=x_codes[:, c, :].bitcast(FP8X4),
-                rhs_scale=x_scales[:, c, :],
-                start=(c == 0),
-                stop=(c == PASSES - 1),
-            )
 
 
 def sum_squares(nc, pools, proj, width, q_t, first_slot, first_col):
@@ -252,22 +283,27 @@ def normalise_rows(nc, pools, ident, q_t, out):
 def tile_texture_encoder_pa_k_kernel(tc, x3, x4, w1_3, w1_4, out):
     nc = tc.nc
     with ExitStack() as ctx:
-        pools = {
-            "const": ctx.enter_context(tc.tile_pool(name="const", bufs=1)),
-            "x_keep": ctx.enter_context(tc.tile_pool(name="x_keep", bufs=1)),
-            "x_stage": ctx.enter_context(tc.tile_pool(name="x_stage", bufs=2)),
-            "w": ctx.enter_context(tc.tile_pool(name="w", bufs=4)),
-            "best": ctx.enter_context(tc.tile_pool(name="best", bufs=2)),
-            "e": ctx.enter_context(tc.tile_pool(name="e", bufs=LANES * CHUNKS + LANES)),
-            "sm": ctx.enter_context(tc.tile_pool(name="sm", bufs=2)),
-            "codes": ctx.enter_context(tc.tile_pool(name="codes", bufs=4)),
-            "row": ctx.enter_context(tc.tile_pool(name="row", bufs=3)),
-            "stats": ctx.enter_context(tc.tile_pool(name="stats", bufs=2)),
-            "psum_w": ctx.enter_context(tc.psum_pool(name="psum_w", bufs=3)),
-            "psum_back": ctx.enter_context(tc.psum_pool(name="psum_back", bufs=2)),
-            "psum_proj": ctx.enter_context(tc.psum_pool(name="psum_proj", bufs=2)),
-            "psum_small": ctx.enter_context(tc.psum_pool(name="psum_small", bufs=1)),
+        sbuf_pools = {
+            "const": 1,
+            "x_keep": 1,
+            "x_raw": 3,
+            "x_grouped": 3,
+            "w": W_AHEAD + 1,
+            "best": 2,
+            "e": LANES * CHUNKS + LANES,
+            "sm_t": LANES,
+            "sm_grouped": LANES,
+            "codes": 2 * LANES,
+            "row": 3,
+            "stats": 2,
         }
+        psum_pools = {"psum_w": 3, "psum_back": 2, "psum_proj": LANES, "psum_small": 1}
+        pools = {}
+        for name, bufs in sbuf_pools.items():
+            pools[name] = ctx.enter_context(tc.tile_pool(name=name, bufs=bufs))
+        for name, bufs in psum_pools.items():
+            pools[name] = ctx.enter_context(tc.psum_pool(name=name, bufs=bufs))
+
         ident = pools["const"].tile([P, P], F32, name="ident")
         make_identity(nc, ident[:])
         q_t = pools["const"].tile([P, 2 * GROUPS, P], F32, name="q_t")
@@ -283,38 +319,91 @@ def tile_texture_encoder_pa_k_kernel(tc, x3, x4, w1_3, w1_4, out):
             jobs.append((w1_4, group, x4_codes, x4_scales, 16, SAMPLES))
         for group in range(GROUPS):
             jobs.append((w1_3, group, x3_codes, x3_scales, 64, 0))
+        steps = len(jobs) * CHUNKS
 
-        statistics = group_statistics(pools)
-        e_tiles = [
-            exponentials(nc, pools, ident, jobs[0][0], jobs[0][1], chunk, statistics)
-            for chunk in range(CHUNKS)
-        ]
-        for first in range(0, PASSES, 4):
-            quantise_x_tile(nc, pools["x_stage"], x4, 16, x4_codes, x4_scales, first)
-        for index in range(len(jobs)):
-            group, x_codes, x_scales, positions, first_col = jobs[index][1:]
-            width = SAMPLES * positions
-            more = index + 1 < len(jobs)
-            next_tiles = []
-            if more:
-                next_w, next_group = jobs[index + 1][0], jobs[index + 1][1]
-                next_statistics = group_statistics(pools)
-                next_tiles.append(exponentials(nc, pools, ident, next_w, next_group, 0, next_statistics))
-            gain = column_gain(nc, pools, statistics)
-            proj = [
-                pools["psum_proj"].tile([P, COLUMNS], F32, name="proj%d" % lane, tag="proj")
-                for lane in range(LANES)
+        x_tiles = {}
+        for c in range(PASSES):
+            x_tiles[c - 1] = [(x3, 64, x3_codes, x3_scales, c)]
+        for i in range(4):
+            x_tiles[X4_FIRST_STEP + i].append((x4, 16, x4_codes, x4_scales, 4 * i))
+
+        w_chunks, w_ts, statistics, rescales, gains = {}, {}, {}, {}, {}
+        e_tiles, sm_groups, projs, x_raws, x_groups = {}, {}, {}, {}, {}
+
+        for s in range(-W_AHEAD, steps + STAGE3_LAG + 1):
+            if s + W_AHEAD < steps:
+                w, group = jobs[(s + W_AHEAD) // CHUNKS][0:2]
+                w_chunks[s + W_AHEAD] = load_w_chunk(nc, pools, w, group, (s + W_AHEAD) % CHUNKS)
+
+            done = s - STAGE3_LAG
+            if 0 <= done < steps:
+                job, chunk = done // CHUNKS, done % CHUNKS
+                x_codes, x_scales, positions, first_col = jobs[job][2:6]
+                width = SAMPLES * positions
+                if chunk == 0:
+                    projs[job] = [
+                        pools["psum_proj"].tile([P, COLUMNS], F32, name="proj%d" % lane, tag="proj")
+                        for lane in range(LANES)
+                    ]
+                quantised = [quantise_sm(nc, pools, grouped) for grouped in sm_groups[done]]
+                for lane in range(LANES):
+                    sm_codes, sm_scales = quantised[lane]
+                    multiply(nc, projs[job][lane][:, 0:width], sm_codes, sm_scales, x_codes, x_scales, chunk)
+
+            mid = s - STAGE2_LAG
+            has_mid = 0 <= mid < steps
+            has_new = 0 <= s < steps
+            if has_mid:
+                job, chunk = mid // CHUNKS, mid % CHUNKS
+                if chunk == 0:
+                    gains[job] = column_gain(nc, pools, statistics[job], rescales[job])
+                sm_ts = [
+                    normalise(nc, pools, e_tiles[mid][lane], gains[job][:, lane, chunk : chunk + 1])
+                    for lane in range(LANES)
+                ]
+                sm_groups[mid] = []
+            if has_new:
+                job, chunk = s // CHUNKS, s % CHUNKS
+                e_tiles[s] = [
+                    pools["e"].tile([P, CHUNK_CHANNELS], F32, name="e_lane%d" % lane, tag="e_tile")
+                    for lane in range(LANES)
+                ]
+                for l in (0, 1):
+                    exponentials(nc, w_ts[(s, l)], e_tiles[s], statistics[job], chunk, l)
+            if has_mid:
+                sm_groups[mid].append(transpose_back(nc, pools, ident, sm_ts[0]))
+            if has_new:
+                w_ts[(s, 2)] = transpose_pass(nc, pools, ident, w_chunks[s], 2)
+            if has_mid:
+                sm_groups[mid].append(transpose_back(nc, pools, ident, sm_ts[1]))
+            if has_new:
+                w_ts[(s, 3)] = transpose_pass(nc, pools, ident, w_chunks[s], 3)
+                for l in (2, 3):
+                    exponentials(nc, w_ts[(s, l)], e_tiles[s], statistics[job], chunk, l)
+
+            for grouped, (x, positions, codes, scales, first) in zip(x_groups.get(s - 1, []), x_tiles.get(s - 1, [])):
+                quantise_x_tile(nc, grouped, codes, scales, first, positions)
+
+            if 0 <= s + 1 < steps:
+                job, chunk = (s + 1) // CHUNKS, (s + 1) % CHUNKS
+                if chunk == 0:
+                    statistics[job] = group_statistics(pools)
+                chunk_maxima(nc, pools, ident, w_chunks[s + 1], statistics[job], chunk)
+                if chunk == CHUNKS - 1:
+                    rescales[job] = chunk_rescale(nc, pools, statistics[job])
+            x_groups[s] = [
+                regroup_x_tile(nc, pools, raw, tile[1]) for raw, tile in zip(x_raws.get(s, []), x_tiles.get(s, []))
             ]
-            for chunk in range(CHUNKS):
-                project(nc, pools, ident, e_tiles[chunk], gain, chunk, proj, x_codes, x_scales, width)
-                if index < GROUPS:
-                    for first in range(2 * (index * CHUNKS + chunk), 2 * (index * CHUNKS + chunk) + 2):
-                        quantise_x_tile(nc, pools["x_stage"], x3, 64, x3_codes, x3_scales, first)
-                if more and chunk + 1 < CHUNKS:
-                    next_tiles.append(
-                        exponentials(nc, pools, ident, next_w, next_group, chunk + 1, next_statistics)
-                    )
-            sum_squares(nc, pools, proj, width, q_t, LANES * group, first_col)
-            if more:
-                statistics, e_tiles = next_statistics, next_tiles
+            x_raws[s + 1] = [
+                load_x_tile(nc, pools, x, positions, first)
+                for x, positions, codes, scales, first in x_tiles.get(s + 1, [])
+            ]
+            if 0 <= s + 1 < steps:
+                for l in (0, 1):
+                    w_ts[(s + 1, l)] = transpose_pass(nc, pools, ident, w_chunks[s + 1], l)
+
+            if 0 <= done < steps and done % CHUNKS == CHUNKS - 1:
+                job = done // CHUNKS
+                group, positions, first_col = jobs[job][1], jobs[job][4], jobs[job][5]
+                sum_squares(nc, pools, projs[job], SAMPLES * positions, q_t, LANES * group, first_col)
         normalise_rows(nc, pools, ident, q_t, out)

@@ -27,9 +27,10 @@ CHUNKS = PASSES // CHUNK_PASSES
 CHUNK_CHANNELS = CHUNK_PASSES * K_PASS
 QUANT_WIDTH = 2048
 W_AHEAD = 3
+PASSES_AHEAD = 3
 STAGE2_LAG = CHUNKS
 STAGE3_LAG = STAGE2_LAG + 1
-X4_FIRST_STEP = 2
+X4_FIRST_STEP = 4
 GRAD_BOOST = 10.0
 EPS = 1e-8
 
@@ -85,20 +86,25 @@ def load_w_chunk(nc, pools, w, group, chunk):
     return w_chunk
 
 
-def chunk_maxima(nc, pools, ident, w_chunk, statistics, chunk):
-    chunk_max, shift = statistics[0], statistics[1]
-    best = pools["best"].tile([P, 8 * GROUP_COLUMNS], BF16, name="best")
-    nc.vector.tensor_tensor(
-        out=best[:],
-        in0=w_chunk[:, 0:2].rearrange("q l t o -> q (l t o)"),
-        in1=w_chunk[:, 2:4].rearrange("q l t o -> q (l t o)"),
-        op=ALU.max,
-    )
-    for rows in (4, 2, 1):
-        half = rows * GROUP_COLUMNS
+def halve_rows(nc, pools, w_chunk, best, rows):
+    half = rows * GROUP_COLUMNS
+    if best is None:
+        best = pools["best"].tile([P, half], BF16, name="best")
+        nc.vector.tensor_tensor(
+            out=best[:],
+            in0=w_chunk[:, 0:2].rearrange("q l t o -> q (l t o)"),
+            in1=w_chunk[:, 2:4].rearrange("q l t o -> q (l t o)"),
+            op=ALU.max,
+        )
+    else:
         nc.vector.tensor_tensor(
             out=best[:, 0:half], in0=best[:, 0:half], in1=best[:, half : 2 * half], op=ALU.max
         )
+    return best
+
+
+def chunk_maxima(nc, pools, ident, best, statistics, chunk):
+    chunk_max = statistics[0]
     best_t = pools["psum_small"].tile([P, P], F32, name="best_t", tag="small")
     nc.tensor.transpose(best_t[:], best[:, 0:GROUP_COLUMNS].bitcast(F32), ident[:])
     nc.vector.tensor_reduce(
@@ -107,6 +113,10 @@ def chunk_maxima(nc, pools, ident, w_chunk, statistics, chunk):
         axis=AXIS_X,
         op=ALU.max,
     )
+
+
+def chunk_shift(nc, statistics, chunk):
+    chunk_max, shift = statistics[0], statistics[1]
     nc.vector.tensor_scalar(
         out=shift[:, :, chunk],
         in0=chunk_max[:, :, chunk],
@@ -140,7 +150,7 @@ def exponentials(nc, w_t, e_lanes, statistics, chunk, l):
         )
 
 
-def chunk_rescale(nc, pools, statistics):
+def below_column_max(nc, pools, statistics):
     chunk_max = statistics[0]
     shape = [P, LANES, CHUNKS]
     col_max = pools["stats"].tile([P, LANES], F32, name="col_max")
@@ -149,7 +159,11 @@ def chunk_rescale(nc, pools, statistics):
     nc.vector.tensor_tensor(
         out=below[:], in0=chunk_max[:], in1=col_max[:].unsqueeze(2).to_broadcast(shape), op=ALU.subtract
     )
-    rescale = pools["stats"].tile(shape, F32, name="rescale")
+    return below
+
+
+def chunk_rescale(nc, pools, below):
+    rescale = pools["stats"].tile([P, LANES, CHUNKS], F32, name="rescale")
     nc.scalar.activation(out=rescale[:], in_=below[:], func=ACT.Exp, scale=GRAD_BOOST)
     return rescale
 
@@ -219,13 +233,19 @@ def multiply(nc, proj_lane, sm_codes, sm_scales, x_codes, x_scales, chunk):
         )
 
 
-def sum_squares(nc, pools, proj, width, q_t, first_slot, first_col):
+def square(nc, pools, proj, width):
+    squares = []
     for lane in range(LANES):
-        squares = pools["row"].tile([P, COLUMNS], F32, name="squares", tag="row")
-        nc.scalar.activation(out=squares[:, 0:width], in_=proj[lane][:, 0:width], func=ACT.Square)
+        squares.append(pools["row"].tile([P, COLUMNS], F32, name="squares%d" % lane, tag="row"))
+        nc.scalar.activation(out=squares[lane][:, 0:width], in_=proj[lane][:, 0:width], func=ACT.Square)
+    return squares
+
+
+def sum_positions(nc, squares, width, q_t, first_slot, first_col):
+    for lane in range(LANES):
         nc.vector.tensor_reduce(
             out=q_t[:, first_slot + lane, first_col : first_col + SAMPLES],
-            in_=squares[:, 0:width].rearrange("i (n f) -> i n f", n=SAMPLES),
+            in_=squares[lane][:, 0:width].rearrange("i (n f) -> i n f", n=SAMPLES),
             axis=AXIS_X,
             op=ALU.add,
         )
@@ -308,6 +328,8 @@ def tile_texture_encoder_pa_k_kernel(tc, x3, x4, w1_3, w1_4, out):
         make_identity(nc, ident[:])
         q_t = pools["const"].tile([P, 2 * GROUPS, P], F32, name="q_t")
         nc.vector.memset(q_t[:], 0.0)
+        warm = pools["const"].tile([P, 2], F32, name="warm")
+        nc.vector.memset(warm[:], 1.0)
 
         x4_codes = pools["x_keep"].tile([P, PASSES, SAMPLES * 16], U32, name="x4_codes", align_bytes=64)
         x4_scales = pools["x_keep"].tile([P, PASSES, SAMPLES * 16], U8, name="x4_scales", align_bytes=64)
@@ -327,83 +349,100 @@ def tile_texture_encoder_pa_k_kernel(tc, x3, x4, w1_3, w1_4, out):
         for i in range(4):
             x_tiles[X4_FIRST_STEP + i].append((x4, 16, x4_codes, x4_scales, 4 * i))
 
-        w_chunks, w_ts, statistics, rescales, gains = {}, {}, {}, {}, {}
-        e_tiles, sm_groups, projs, x_raws, x_groups = {}, {}, {}, {}, {}
+        w_chunks, bests, w_ts, statistics, belows, rescales, gains = {}, {}, {}, {}, {}, {}, {}
+        e_tiles, sm_ts, sm_groups, quantised, projs, squares, x_raws, x_groups = {}, {}, {}, {}, {}, {}, {}, {}
 
-        for s in range(-W_AHEAD, steps + STAGE3_LAG + 1):
-            if s + W_AHEAD < steps:
-                w, group = jobs[(s + W_AHEAD) // CHUNKS][0:2]
-                w_chunks[s + W_AHEAD] = load_w_chunk(nc, pools, w, group, (s + W_AHEAD) % CHUNKS)
+        with tc.manual_schedule():
+            for s in range(-W_AHEAD, steps + STAGE3_LAG + 3):
+                mid, done = s - STAGE2_LAG, s - STAGE3_LAG
+                has_new, has_mid, has_done = 0 <= s < steps, 0 <= mid < steps, 0 <= done < steps
+                has_next, has_tree = 0 <= s + 1 < steps, 0 <= s + 2 < steps
 
-            done = s - STAGE3_LAG
-            if 0 <= done < steps:
-                job, chunk = done // CHUNKS, done % CHUNKS
-                x_codes, x_scales, positions, first_col = jobs[job][2:6]
-                width = SAMPLES * positions
-                if chunk == 0:
-                    projs[job] = [
-                        pools["psum_proj"].tile([P, COLUMNS], F32, name="proj%d" % lane, tag="proj")
+                if s + W_AHEAD < steps:
+                    w, group = jobs[(s + W_AHEAD) // CHUNKS][0:2]
+                    w_chunks[s + W_AHEAD] = load_w_chunk(nc, pools, w, group, (s + W_AHEAD) % CHUNKS)
+
+                if has_tree:
+                    bests[s + 2] = halve_rows(nc, pools, w_chunks[s + 2], None, 8)
+                if has_done:
+                    quantised[done] = [quantise_sm(nc, pools, sm_groups[done][0])]
+                if has_tree:
+                    halve_rows(nc, pools, w_chunks[s + 2], bests[s + 2], 4)
+                if has_mid:
+                    job, chunk = mid // CHUNKS, mid % CHUNKS
+                    if chunk == 0:
+                        gains[job] = column_gain(nc, pools, statistics[job], rescales[job])
+                    sm_ts[mid] = [normalise(nc, pools, e_tiles[mid][0], gains[job][:, 0, chunk : chunk + 1])]
+                if has_tree:
+                    halve_rows(nc, pools, w_chunks[s + 2], bests[s + 2], 2)
+                if has_mid:
+                    sm_ts[mid].append(normalise(nc, pools, e_tiles[mid][1], gains[job][:, 1, chunk : chunk + 1]))
+                if has_tree:
+                    halve_rows(nc, pools, w_chunks[s + 2], bests[s + 2], 1)
+                if has_done:
+                    quantised[done].append(quantise_sm(nc, pools, sm_groups[done][1]))
+                if has_next:
+                    job, chunk = (s + 1) // CHUNKS, (s + 1) % CHUNKS
+                    if chunk == 0:
+                        statistics[job] = group_statistics(pools)
+                    chunk_maxima(nc, pools, ident, bests[s + 1], statistics[job], chunk)
+                for grouped, tile in zip(x_groups.get(s - 1, []), x_tiles.get(s - 1, [])):
+                    quantise_x_tile(nc, grouped, tile[2], tile[3], tile[4], tile[1])
+                if has_next:
+                    chunk_shift(nc, statistics[job], chunk)
+                    if chunk == CHUNKS - 1:
+                        belows[job] = below_column_max(nc, pools, statistics[job])
+                x_groups[s] = [
+                    regroup_x_tile(nc, pools, raw, tile[1]) for raw, tile in zip(x_raws.get(s, []), x_tiles.get(s, []))
+                ]
+                if 0 <= done - 2 < steps and (done - 2) % CHUNKS == CHUNKS - 1:
+                    ready = (done - 2) // CHUNKS
+                    group, positions, first_col = jobs[ready][1], jobs[ready][4], jobs[ready][5]
+                    sum_positions(nc, squares[ready], SAMPLES * positions, q_t, LANES * group, first_col)
+                x_raws[s + 1] = [
+                    load_x_tile(nc, pools, tile[0], tile[1], tile[4]) for tile in x_tiles.get(s + 1, [])
+                ]
+
+                if has_new:
+                    job, chunk = s // CHUNKS, s % CHUNKS
+                    e_tiles[s] = [
+                        pools["e"].tile([P, CHUNK_CHANNELS], F32, name="e_lane%d" % lane, tag="e_tile")
                         for lane in range(LANES)
                     ]
-                quantised = [quantise_sm(nc, pools, grouped) for grouped in sm_groups[done]]
-                for lane in range(LANES):
-                    sm_codes, sm_scales = quantised[lane]
-                    multiply(nc, projs[job][lane][:, 0:width], sm_codes, sm_scales, x_codes, x_scales, chunk)
+                    for l in range(PASSES_AHEAD):
+                        exponentials(nc, w_ts[(s, l)], e_tiles[s], statistics[job], chunk, l)
+                if has_mid:
+                    sm_groups[mid] = [transpose_back(nc, pools, ident, sm_ts[mid][0])]
+                if 0 <= done - 1 < steps and (done - 1) % CHUNKS == CHUNKS - 1:
+                    ready = (done - 1) // CHUNKS
+                    positions = jobs[ready][4]
+                    squares[ready] = square(nc, pools, projs[ready], SAMPLES * positions)
+                if has_new:
+                    for l in range(PASSES_AHEAD, CHUNK_PASSES):
+                        w_ts[(s, l)] = transpose_pass(nc, pools, ident, w_chunks[s], l)
+                        exponentials(nc, w_ts[(s, l)], e_tiles[s], statistics[job], chunk, l)
+                if has_mid:
+                    sm_groups[mid].append(transpose_back(nc, pools, ident, sm_ts[mid][1]))
+                if has_next and (s + 1) % CHUNKS == CHUNKS - 1:
+                    rescales[(s + 1) // CHUNKS] = chunk_rescale(nc, pools, belows[(s + 1) // CHUNKS])
+                if s == steps - 1:
+                    nc.scalar.activation(out=warm[:, 1:2], in_=warm[:, 0:1], func=ACT.Sqrt)
 
-            mid = s - STAGE2_LAG
-            has_mid = 0 <= mid < steps
-            has_new = 0 <= s < steps
-            if has_mid:
-                job, chunk = mid // CHUNKS, mid % CHUNKS
-                if chunk == 0:
-                    gains[job] = column_gain(nc, pools, statistics[job], rescales[job])
-                sm_ts = [
-                    normalise(nc, pools, e_tiles[mid][lane], gains[job][:, lane, chunk : chunk + 1])
-                    for lane in range(LANES)
-                ]
-                sm_groups[mid] = []
-            if has_new:
-                job, chunk = s // CHUNKS, s % CHUNKS
-                e_tiles[s] = [
-                    pools["e"].tile([P, CHUNK_CHANNELS], F32, name="e_lane%d" % lane, tag="e_tile")
-                    for lane in range(LANES)
-                ]
-                for l in (0, 1):
-                    exponentials(nc, w_ts[(s, l)], e_tiles[s], statistics[job], chunk, l)
-            if has_mid:
-                sm_groups[mid].append(transpose_back(nc, pools, ident, sm_ts[0]))
-            if has_new:
-                w_ts[(s, 2)] = transpose_pass(nc, pools, ident, w_chunks[s], 2)
-            if has_mid:
-                sm_groups[mid].append(transpose_back(nc, pools, ident, sm_ts[1]))
-            if has_new:
-                w_ts[(s, 3)] = transpose_pass(nc, pools, ident, w_chunks[s], 3)
-                for l in (2, 3):
-                    exponentials(nc, w_ts[(s, l)], e_tiles[s], statistics[job], chunk, l)
-
-            for grouped, (x, positions, codes, scales, first) in zip(x_groups.get(s - 1, []), x_tiles.get(s - 1, [])):
-                quantise_x_tile(nc, grouped, codes, scales, first, positions)
-
-            if 0 <= s + 1 < steps:
-                job, chunk = (s + 1) // CHUNKS, (s + 1) % CHUNKS
-                if chunk == 0:
-                    statistics[job] = group_statistics(pools)
-                chunk_maxima(nc, pools, ident, w_chunks[s + 1], statistics[job], chunk)
-                if chunk == CHUNKS - 1:
-                    rescales[job] = chunk_rescale(nc, pools, statistics[job])
-            x_groups[s] = [
-                regroup_x_tile(nc, pools, raw, tile[1]) for raw, tile in zip(x_raws.get(s, []), x_tiles.get(s, []))
-            ]
-            x_raws[s + 1] = [
-                load_x_tile(nc, pools, x, positions, first)
-                for x, positions, codes, scales, first in x_tiles.get(s + 1, [])
-            ]
-            if 0 <= s + 1 < steps:
-                for l in (0, 1):
-                    w_ts[(s + 1, l)] = transpose_pass(nc, pools, ident, w_chunks[s + 1], l)
-
-            if 0 <= done < steps and done % CHUNKS == CHUNKS - 1:
-                job = done // CHUNKS
-                group, positions, first_col = jobs[job][1], jobs[job][4], jobs[job][5]
-                sum_squares(nc, pools, projs[job], SAMPLES * positions, q_t, LANES * group, first_col)
-        normalise_rows(nc, pools, ident, q_t, out)
+                if has_done:
+                    job, chunk = done // CHUNKS, done % CHUNKS
+                    x_codes, x_scales, positions = jobs[job][2:5]
+                    if chunk == 0:
+                        projs[job] = [
+                            pools["psum_proj"].tile([P, COLUMNS], F32, name="proj%d" % lane, tag="proj")
+                            for lane in range(LANES)
+                        ]
+                    for lane in range(LANES):
+                        sm_codes, sm_scales = quantised[done][lane]
+                        multiply(
+                            nc, projs[job][lane][:, 0 : SAMPLES * positions], sm_codes, sm_scales,
+                            x_codes, x_scales, chunk,
+                        )
+                if has_next:
+                    for l in range(PASSES_AHEAD):
+                        w_ts[(s + 1, l)] = transpose_pass(nc, pools, ident, w_chunks[s + 1], l)
+            normalise_rows(nc, pools, ident, q_t, out)

@@ -328,8 +328,7 @@ def tile_texture_encoder_pa_k_kernel(tc, x3, x4, w1_3, w1_4, out):
         make_identity(nc, ident[:])
         q_t = pools["const"].tile([P, 2 * GROUPS, P], F32, name="q_t")
         nc.vector.memset(q_t[:], 0.0)
-        warm = pools["const"].tile([P, 2], F32, name="warm")
-        nc.vector.memset(warm[:], 1.0)
+        warm = pools["const"].tile([P, 1], F32, name="warm")
 
         x4_codes = pools["x_keep"].tile([P, PASSES, SAMPLES * 16], U32, name="x4_codes", align_bytes=64)
         x4_scales = pools["x_keep"].tile([P, PASSES, SAMPLES * 16], U8, name="x4_scales", align_bytes=64)
@@ -352,97 +351,96 @@ def tile_texture_encoder_pa_k_kernel(tc, x3, x4, w1_3, w1_4, out):
         w_chunks, bests, w_ts, statistics, belows, rescales, gains = {}, {}, {}, {}, {}, {}, {}
         e_tiles, sm_ts, sm_groups, quantised, projs, squares, x_raws, x_groups = {}, {}, {}, {}, {}, {}, {}, {}
 
-        with tc.manual_schedule():
-            for s in range(-W_AHEAD, steps + STAGE3_LAG + 3):
-                mid, done = s - STAGE2_LAG, s - STAGE3_LAG
-                has_new, has_mid, has_done = 0 <= s < steps, 0 <= mid < steps, 0 <= done < steps
-                has_next, has_tree = 0 <= s + 1 < steps, 0 <= s + 2 < steps
+        for s in range(-W_AHEAD, steps + STAGE3_LAG + 3):
+            mid, done = s - STAGE2_LAG, s - STAGE3_LAG
+            has_new, has_mid, has_done = 0 <= s < steps, 0 <= mid < steps, 0 <= done < steps
+            has_next, has_tree = 0 <= s + 1 < steps, 0 <= s + 2 < steps
 
-                if s + W_AHEAD < steps:
-                    w, group = jobs[(s + W_AHEAD) // CHUNKS][0:2]
-                    w_chunks[s + W_AHEAD] = load_w_chunk(nc, pools, w, group, (s + W_AHEAD) % CHUNKS)
+            if s + W_AHEAD < steps:
+                w, group = jobs[(s + W_AHEAD) // CHUNKS][0:2]
+                w_chunks[s + W_AHEAD] = load_w_chunk(nc, pools, w, group, (s + W_AHEAD) % CHUNKS)
 
-                if has_tree:
-                    bests[s + 2] = halve_rows(nc, pools, w_chunks[s + 2], None, 8)
-                if has_done:
-                    quantised[done] = [quantise_sm(nc, pools, sm_groups[done][0])]
-                if has_tree:
-                    halve_rows(nc, pools, w_chunks[s + 2], bests[s + 2], 4)
-                if has_mid:
-                    job, chunk = mid // CHUNKS, mid % CHUNKS
-                    if chunk == 0:
-                        gains[job] = column_gain(nc, pools, statistics[job], rescales[job])
-                    sm_ts[mid] = [normalise(nc, pools, e_tiles[mid][0], gains[job][:, 0, chunk : chunk + 1])]
-                if has_tree:
-                    halve_rows(nc, pools, w_chunks[s + 2], bests[s + 2], 2)
-                if has_mid:
-                    sm_ts[mid].append(normalise(nc, pools, e_tiles[mid][1], gains[job][:, 1, chunk : chunk + 1]))
-                if has_tree:
-                    halve_rows(nc, pools, w_chunks[s + 2], bests[s + 2], 1)
-                if has_done:
-                    quantised[done].append(quantise_sm(nc, pools, sm_groups[done][1]))
-                if has_next:
-                    job, chunk = (s + 1) // CHUNKS, (s + 1) % CHUNKS
-                    if chunk == 0:
-                        statistics[job] = group_statistics(pools)
-                    chunk_maxima(nc, pools, ident, bests[s + 1], statistics[job], chunk)
-                for grouped, tile in zip(x_groups.get(s - 1, []), x_tiles.get(s - 1, [])):
-                    quantise_x_tile(nc, grouped, tile[2], tile[3], tile[4], tile[1])
-                if has_next:
-                    chunk_shift(nc, statistics[job], chunk)
-                    if chunk == CHUNKS - 1:
-                        belows[job] = below_column_max(nc, pools, statistics[job])
-                x_groups[s] = [
-                    regroup_x_tile(nc, pools, raw, tile[1]) for raw, tile in zip(x_raws.get(s, []), x_tiles.get(s, []))
+            if has_tree:
+                bests[s + 2] = halve_rows(nc, pools, w_chunks[s + 2], None, 8)
+            if has_done:
+                quantised[done] = [quantise_sm(nc, pools, sm_groups[done][0])]
+            if has_tree:
+                halve_rows(nc, pools, w_chunks[s + 2], bests[s + 2], 4)
+            if has_mid:
+                job, chunk = mid // CHUNKS, mid % CHUNKS
+                if chunk == 0:
+                    gains[job] = column_gain(nc, pools, statistics[job], rescales[job])
+                sm_ts[mid] = [normalise(nc, pools, e_tiles[mid][0], gains[job][:, 0, chunk : chunk + 1])]
+            if has_tree:
+                halve_rows(nc, pools, w_chunks[s + 2], bests[s + 2], 2)
+            if has_mid:
+                sm_ts[mid].append(normalise(nc, pools, e_tiles[mid][1], gains[job][:, 1, chunk : chunk + 1]))
+            if has_tree:
+                halve_rows(nc, pools, w_chunks[s + 2], bests[s + 2], 1)
+            if has_done:
+                quantised[done].append(quantise_sm(nc, pools, sm_groups[done][1]))
+            if has_next:
+                job, chunk = (s + 1) // CHUNKS, (s + 1) % CHUNKS
+                if chunk == 0:
+                    statistics[job] = group_statistics(pools)
+                chunk_maxima(nc, pools, ident, bests[s + 1], statistics[job], chunk)
+            for grouped, tile in zip(x_groups.get(s - 1, []), x_tiles.get(s - 1, [])):
+                quantise_x_tile(nc, grouped, tile[2], tile[3], tile[4], tile[1])
+            if has_next:
+                chunk_shift(nc, statistics[job], chunk)
+                if chunk == CHUNKS - 1:
+                    belows[job] = below_column_max(nc, pools, statistics[job])
+            x_groups[s] = [
+                regroup_x_tile(nc, pools, raw, tile[1]) for raw, tile in zip(x_raws.get(s, []), x_tiles.get(s, []))
+            ]
+            if 0 <= done - 2 < steps and (done - 2) % CHUNKS == CHUNKS - 1:
+                ready = (done - 2) // CHUNKS
+                group, positions, first_col = jobs[ready][1], jobs[ready][4], jobs[ready][5]
+                sum_positions(nc, squares[ready], SAMPLES * positions, q_t, LANES * group, first_col)
+            x_raws[s + 1] = [
+                load_x_tile(nc, pools, tile[0], tile[1], tile[4]) for tile in x_tiles.get(s + 1, [])
+            ]
+
+            if has_new:
+                job, chunk = s // CHUNKS, s % CHUNKS
+                e_tiles[s] = [
+                    pools["e"].tile([P, CHUNK_CHANNELS], F32, name="e_lane%d" % lane, tag="e_tile")
+                    for lane in range(LANES)
                 ]
-                if 0 <= done - 2 < steps and (done - 2) % CHUNKS == CHUNKS - 1:
-                    ready = (done - 2) // CHUNKS
-                    group, positions, first_col = jobs[ready][1], jobs[ready][4], jobs[ready][5]
-                    sum_positions(nc, squares[ready], SAMPLES * positions, q_t, LANES * group, first_col)
-                x_raws[s + 1] = [
-                    load_x_tile(nc, pools, tile[0], tile[1], tile[4]) for tile in x_tiles.get(s + 1, [])
-                ]
+                for l in range(PASSES_AHEAD):
+                    exponentials(nc, w_ts[(s, l)], e_tiles[s], statistics[job], chunk, l)
+            if has_mid:
+                sm_groups[mid] = [transpose_back(nc, pools, ident, sm_ts[mid][0])]
+            if 0 <= done - 1 < steps and (done - 1) % CHUNKS == CHUNKS - 1:
+                ready = (done - 1) // CHUNKS
+                positions = jobs[ready][4]
+                squares[ready] = square(nc, pools, projs[ready], SAMPLES * positions)
+            if has_new:
+                for l in range(PASSES_AHEAD, CHUNK_PASSES):
+                    w_ts[(s, l)] = transpose_pass(nc, pools, ident, w_chunks[s], l)
+                    exponentials(nc, w_ts[(s, l)], e_tiles[s], statistics[job], chunk, l)
+            if has_mid:
+                sm_groups[mid].append(transpose_back(nc, pools, ident, sm_ts[mid][1]))
+            if has_next and (s + 1) % CHUNKS == CHUNKS - 1:
+                rescales[(s + 1) // CHUNKS] = chunk_rescale(nc, pools, belows[(s + 1) // CHUNKS])
+            if s == steps - 1:
+                nc.scalar.activation(out=warm[:], in_=statistics[job][2][:, LANES - 1, chunk, CHUNK_PASSES - 1 :], func=ACT.Sqrt)
 
-                if has_new:
-                    job, chunk = s // CHUNKS, s % CHUNKS
-                    e_tiles[s] = [
-                        pools["e"].tile([P, CHUNK_CHANNELS], F32, name="e_lane%d" % lane, tag="e_tile")
+            if has_done:
+                job, chunk = done // CHUNKS, done % CHUNKS
+                x_codes, x_scales, positions = jobs[job][2:5]
+                if chunk == 0:
+                    projs[job] = [
+                        pools["psum_proj"].tile([P, COLUMNS], F32, name="proj%d" % lane, tag="proj")
                         for lane in range(LANES)
                     ]
-                    for l in range(PASSES_AHEAD):
-                        exponentials(nc, w_ts[(s, l)], e_tiles[s], statistics[job], chunk, l)
-                if has_mid:
-                    sm_groups[mid] = [transpose_back(nc, pools, ident, sm_ts[mid][0])]
-                if 0 <= done - 1 < steps and (done - 1) % CHUNKS == CHUNKS - 1:
-                    ready = (done - 1) // CHUNKS
-                    positions = jobs[ready][4]
-                    squares[ready] = square(nc, pools, projs[ready], SAMPLES * positions)
-                if has_new:
-                    for l in range(PASSES_AHEAD, CHUNK_PASSES):
-                        w_ts[(s, l)] = transpose_pass(nc, pools, ident, w_chunks[s], l)
-                        exponentials(nc, w_ts[(s, l)], e_tiles[s], statistics[job], chunk, l)
-                if has_mid:
-                    sm_groups[mid].append(transpose_back(nc, pools, ident, sm_ts[mid][1]))
-                if has_next and (s + 1) % CHUNKS == CHUNKS - 1:
-                    rescales[(s + 1) // CHUNKS] = chunk_rescale(nc, pools, belows[(s + 1) // CHUNKS])
-                if s == steps - 1:
-                    nc.scalar.activation(out=warm[:, 1:2], in_=warm[:, 0:1], func=ACT.Sqrt)
-
-                if has_done:
-                    job, chunk = done // CHUNKS, done % CHUNKS
-                    x_codes, x_scales, positions = jobs[job][2:5]
-                    if chunk == 0:
-                        projs[job] = [
-                            pools["psum_proj"].tile([P, COLUMNS], F32, name="proj%d" % lane, tag="proj")
-                            for lane in range(LANES)
-                        ]
-                    for lane in range(LANES):
-                        sm_codes, sm_scales = quantised[done][lane]
-                        multiply(
-                            nc, projs[job][lane][:, 0 : SAMPLES * positions], sm_codes, sm_scales,
-                            x_codes, x_scales, chunk,
-                        )
-                if has_next:
-                    for l in range(PASSES_AHEAD):
-                        w_ts[(s + 1, l)] = transpose_pass(nc, pools, ident, w_chunks[s + 1], l)
-            normalise_rows(nc, pools, ident, q_t, out)
+                for lane in range(LANES):
+                    sm_codes, sm_scales = quantised[done][lane]
+                    multiply(
+                        nc, projs[job][lane][:, 0 : SAMPLES * positions], sm_codes, sm_scales,
+                        x_codes, x_scales, chunk,
+                    )
+            if has_next:
+                for l in range(PASSES_AHEAD):
+                    w_ts[(s + 1, l)] = transpose_pass(nc, pools, ident, w_chunks[s + 1], l)
+        normalise_rows(nc, pools, ident, q_t, out)

@@ -257,29 +257,13 @@ def normalise_rows(nc, pools, ident, q_t, out):
     for slot in range(2 * GROUPS):
         nc.tensor.transpose(q_rows[:, slot, :], q_t[:, slot, :], ident[:])
     stats = pools["stats"]
-    mean = stats.tile([P, 1], F32, name="mean")
-    nc.vector.tensor_reduce(
-        out=mean[0:rows], in_=q_rows[0:rows].rearrange("r s i -> r (s i)"), axis=AXIS_X, op=ALU.add
-    )
-    nc.vector.tensor_scalar(
-        out=mean[0:rows], in0=mean[0:rows], scalar1=1.0 / COLUMNS, scalar2=None, op0=ALU.mult
-    )
-    centred = pools["row"].tile([P, COLUMNS], F32, name="centred", tag="row")
-    nc.vector.tensor_scalar(
-        out=centred[0:rows].rearrange("r (g i e) -> r g i e", g=GROUPS, e=LANES),
-        in0=q_rows[0:rows].rearrange("r (g e) i -> r g i e", e=LANES),
-        scalar1=mean[0:rows, 0:1],
-        scalar2=None,
-        op0=ALU.subtract,
-    )
-    squares = pools["row"].tile([P, COLUMNS], F32, name="dev_squares", tag="row")
-    spread = stats.tile([P, 1], F32, name="spread")
-    nc.scalar.activation(
-        out=squares[0:rows], in_=centred[0:rows], func=ACT.Square, accum_out=spread[0:rows, 0:1]
-    )
+    moments = stats.tile([P, 6], F32, name="moments")
+    nc.vector.bn_stats(out=moments[0:rows], in_=q_rows[0:rows].rearrange("r s i -> r (s i)"))
+    mean_var = stats.tile([P, 2], F32, name="mean_var")
+    nc.vector.bn_aggr(out=mean_var[0:rows], in_=moments[0:rows])
     std = stats.tile([P, 1], F32, name="std")
     nc.scalar.activation(
-        out=std[0:rows], in_=spread[0:rows], func=ACT.Sqrt, scale=1.0 / (COLUMNS - 1)
+        out=std[0:rows], in_=mean_var[0:rows, 1:2], func=ACT.Sqrt, scale=COLUMNS / (COLUMNS - 1.0)
     )
     inverse = stats.tile([P, 1], F32, name="inverse")
     nc.vector.tensor_scalar(
@@ -288,11 +272,12 @@ def normalise_rows(nc, pools, ident, q_t, out):
     nc.vector.reciprocal(out=inverse[0:rows], in_=inverse[0:rows])
     result = pools["row"].tile([P, COLUMNS], F32, name="result", tag="row")
     nc.vector.tensor_scalar(
-        out=result[0:rows],
-        in0=centred[0:rows],
-        scalar1=inverse[0:rows, 0:1],
-        scalar2=None,
-        op0=ALU.mult,
+        out=result[0:rows].rearrange("r (g i e) -> r g i e", g=GROUPS, e=LANES),
+        in0=q_rows[0:rows].rearrange("r (g e) i -> r g i e", e=LANES),
+        scalar1=mean_var[0:rows, 0:1],
+        scalar2=inverse[0:rows, 0:1],
+        op0=ALU.subtract,
+        op1=ALU.mult,
     )
     for s in range(2):
         nc.sync.dma_start(

@@ -32,6 +32,8 @@ STAGE2_LAG = CHUNKS
 STAGE3_LAG = STAGE2_LAG + 1
 X4_FIRST_STEP = 4
 GRAD_BOOST = 10.0
+SHARED_STEPS = 11
+SCALAR_SHARE = 512
 EPS = 1e-8
 
 FLOPS = 2 * SAMPLES * (64 + 16) * CHANNELS * COLUMNS
@@ -48,10 +50,10 @@ def load_x_tile(nc, pools, x, positions, first):
     return raw
 
 
-def regroup_x_tile(nc, pools, raw, positions):
+def regroup_x_tile(nc, pools, raw, positions, copy):
     grouped = pools["x_grouped"].tile([P, QUANT_WIDTH // (PACK * positions), positions, PACK], BF16,
                                       name="x_grouped", align_bytes=64)
-    nc.vector.tensor_copy(
+    copy(
         out=grouped[:].rearrange("q a (c i) t -> q a c t i", i=4),
         in_=raw[:].rearrange("q l n (t c i) -> q (l n) c t i", t=PACK, i=4),
     )
@@ -184,11 +186,14 @@ def column_gain(nc, pools, statistics, rescale):
     return gain
 
 
-def normalise(nc, pools, e_lane, gain_column):
+def normalise(nc, pools, e_lane, gain_column, on_scalar):
     sm_t = pools["sm_t"].tile([P, CHUNK_CHANNELS], BF16, name="sm_t")
+    cut = CHUNK_CHANNELS - on_scalar
     nc.vector.tensor_scalar(
-        out=sm_t[:], in0=e_lane[:], scalar1=gain_column, scalar2=None, op0=ALU.mult
+        out=sm_t[:, 0:cut], in0=e_lane[:, 0:cut], scalar1=gain_column, scalar2=None, op0=ALU.mult
     )
+    if on_scalar:
+        nc.scalar.activation(out=sm_t[:, cut:], in_=e_lane[:, cut:], func=ACT.Copy, scale=gain_column)
     return sm_t
 
 
@@ -309,11 +314,15 @@ def tile_texture_encoder_pa_k_kernel(tc, x3, x4, w1_3, w1_4, out):
         for name, bufs in psum_pools.items():
             pools[name] = ctx.enter_context(tc.psum_pool(name=name, bufs=bufs))
 
+        ctx.enter_context(tc.manual_schedule(engines={mybir.EngineType.SP}))
+
         ident = pools["const"].tile([P, P], F32, name="ident")
         make_identity(nc, ident[:])
         q_t = pools["const"].tile([P, 2 * GROUPS, P], F32, name="q_t")
         nc.vector.memset(q_t[:], 0.0)
         warm = pools["const"].tile([P, 1], F32, name="warm")
+        nc.vector.memset(warm[:], 0.0)
+        nc.scalar.activation(out=warm[:], in_=warm[:], func=ACT.Exp)
 
         x4_codes = pools["x_keep"].tile([P, PASSES, SAMPLES * 16], U32, name="x4_codes", align_bytes=64)
         x4_scales = pools["x_keep"].tile([P, PASSES, SAMPLES * 16], U8, name="x4_scales", align_bytes=64)
@@ -347,36 +356,38 @@ def tile_texture_encoder_pa_k_kernel(tc, x3, x4, w1_3, w1_4, out):
 
             if has_tree:
                 bests[s + 2] = halve_rows(nc, pools, w_chunks[s + 2], None, 8)
-            if has_done:
-                quantised[done] = [quantise_sm(nc, pools, sm_groups[done][0])]
-            if has_tree:
-                halve_rows(nc, pools, w_chunks[s + 2], bests[s + 2], 4)
-            if has_mid:
-                job, chunk = mid // CHUNKS, mid % CHUNKS
-                if chunk == 0:
-                    gains[job] = column_gain(nc, pools, statistics[job], rescales[job])
-                sm_ts[mid] = [normalise(nc, pools, e_tiles[mid][0], gains[job][:, 0, chunk : chunk + 1])]
-            if has_tree:
-                halve_rows(nc, pools, w_chunks[s + 2], bests[s + 2], 2)
-            if has_mid:
-                sm_ts[mid].append(normalise(nc, pools, e_tiles[mid][1], gains[job][:, 1, chunk : chunk + 1]))
-            if has_tree:
-                halve_rows(nc, pools, w_chunks[s + 2], bests[s + 2], 1)
-            if has_done:
-                quantised[done].append(quantise_sm(nc, pools, sm_groups[done][1]))
             if has_next:
                 job, chunk = (s + 1) // CHUNKS, (s + 1) % CHUNKS
                 if chunk == 0:
                     statistics[job] = group_statistics(pools)
                 chunk_maxima(nc, pools, ident, bests[s + 1], statistics[job], chunk)
-            for grouped, tile in zip(x_groups.get(s - 1, []), x_tiles.get(s - 1, [])):
-                quantise_x_tile(nc, grouped, tile[2], tile[3], tile[4], tile[1])
+            if has_done:
+                quantised[done] = [quantise_sm(nc, pools, sm_groups[done][0])]
+            if has_tree:
+                halve_rows(nc, pools, w_chunks[s + 2], bests[s + 2], 4)
             if has_next:
+                job, chunk = (s + 1) // CHUNKS, (s + 1) % CHUNKS
                 chunk_shift(nc, statistics[job], chunk)
                 if chunk == CHUNKS - 1:
                     belows[job] = below_column_max(nc, pools, statistics[job])
+            if has_mid:
+                job, chunk = mid // CHUNKS, mid % CHUNKS
+                if chunk == 0:
+                    gains[job] = column_gain(nc, pools, statistics[job], rescales[job])
+                sm_ts[mid] = [normalise(nc, pools, e_tiles[mid][0], gains[job][:, 0, chunk : chunk + 1], 0)]
+            if has_tree:
+                halve_rows(nc, pools, w_chunks[s + 2], bests[s + 2], 2)
+            if has_mid:
+                sm_ts[mid].append(normalise(nc, pools, e_tiles[mid][1], gains[job][:, 1, chunk : chunk + 1], SCALAR_SHARE if mid < SHARED_STEPS else 0))
+            if has_tree:
+                halve_rows(nc, pools, w_chunks[s + 2], bests[s + 2], 1)
+            if has_done:
+                quantised[done].append(quantise_sm(nc, pools, sm_groups[done][1]))
+            for grouped, tile in zip(x_groups.get(s - 1, []), x_tiles.get(s - 1, [])):
+                quantise_x_tile(nc, grouped, tile[2], tile[3], tile[4], tile[1])
             x_groups[s] = [
-                regroup_x_tile(nc, pools, raw, tile[1]) for raw, tile in zip(x_raws.get(s, []), x_tiles.get(s, []))
+                regroup_x_tile(nc, pools, raw, tile[1], nc.vector.tensor_copy)
+                for raw, tile in zip(x_raws.get(s, []), x_tiles.get(s, []))
             ]
             if 0 <= done - 2 < steps and (done - 2) % CHUNKS == CHUNKS - 1:
                 ready = (done - 2) // CHUNKS

@@ -119,12 +119,8 @@ def chunk_maxima(nc, pools, ident, best, statistics, chunk):
 
 def chunk_shift(nc, statistics, chunk):
     chunk_max, shift = statistics[0], statistics[1]
-    nc.vector.tensor_scalar(
-        out=shift[:, :, chunk],
-        in0=chunk_max[:, :, chunk],
-        scalar1=-GRAD_BOOST,
-        scalar2=None,
-        op0=ALU.mult,
+    nc.scalar.activation(
+        out=shift[:, :, chunk], in_=chunk_max[:, :, chunk], func=ACT.Copy, scale=-GRAD_BOOST
     )
 
 
@@ -338,13 +334,15 @@ def tile_texture_encoder_pa_k_kernel(tc, x3, x4, w1_3, w1_4, out):
 
         x_tiles = {}
         for c in range(PASSES):
-            x_tiles[c - 1] = [(x3, 64, x3_codes, x3_scales, c)]
+            x_tiles[c - 1 if c else -2] = [(x3, 64, x3_codes, x3_scales, c)]
         for i in range(4):
             x_tiles[X4_FIRST_STEP + i].append((x4, 16, x4_codes, x4_scales, 4 * i))
 
         w_chunks, bests, w_ts, statistics, belows, rescales, gains = {}, {}, {}, {}, {}, {}, {}
         e_tiles, sm_ts, sm_groups, quantised, projs, squares, x_raws, x_groups = {}, {}, {}, {}, {}, {}, {}, {}
 
+        first_tile = x_tiles[-2][0]
+        x_raws[-2] = [load_x_tile(nc, pools, first_tile[0], first_tile[1], first_tile[4])]
         for s in range(-W_AHEAD, steps + STAGE3_LAG + 3):
             mid, done = s - STAGE2_LAG, s - STAGE3_LAG
             has_new, has_mid, has_done = 0 <= s < steps, 0 <= mid < steps, 0 <= done < steps
@@ -393,9 +391,10 @@ def tile_texture_encoder_pa_k_kernel(tc, x3, x4, w1_3, w1_4, out):
                 ready = (done - 2) // CHUNKS
                 group, positions, first_col = jobs[ready][1], jobs[ready][4], jobs[ready][5]
                 sum_positions(nc, squares[ready], SAMPLES * positions, q_t, LANES * group, first_col)
-            x_raws[s + 1] = [
-                load_x_tile(nc, pools, tile[0], tile[1], tile[4]) for tile in x_tiles.get(s + 1, [])
-            ]
+            if s + 1 not in x_raws:
+                x_raws[s + 1] = [
+                    load_x_tile(nc, pools, tile[0], tile[1], tile[4]) for tile in x_tiles.get(s + 1, [])
+                ]
 
             if has_new:
                 job, chunk = s // CHUNKS, s % CHUNKS

from contextlib import ExitStack

import concourse.mybir as mybir
from concourse.masks import make_identity

F32 = mybir.dt.float32
BF16 = mybir.dt.bfloat16
U32 = mybir.dt.uint32
U8 = mybir.dt.uint8
FP8X4 = mybir.dt.float8_e4m3fn_x4
ALU = mybir.AluOpType
ACT = mybir.ActivationFunctionType
AXIS_X = mybir.AxisListType.X

P = 128
PACK = 4
K_PASS = P * PACK
CHANNELS = 8192
PASSES = CHANNELS // K_PASS
SAMPLES = 8
COLUMNS = 512
LANES = 2
GROUP_COLUMNS = P * LANES
GROUPS = COLUMNS // GROUP_COLUMNS
CHUNK_PASSES = 4
CHUNKS = PASSES // CHUNK_PASSES
CHUNK_CHANNELS = CHUNK_PASSES * K_PASS
QUANT_WIDTH = 2048
W_AHEAD = 3
PASSES_AHEAD = 3
STAGE2_LAG = CHUNKS
STAGE3_LAG = STAGE2_LAG + 1
X4_FIRST_STEP = 4
GRAD_BOOST = 10.0
SHARED_STEPS = 11
SCALAR_SHARE = 512
EPS = 1e-8

FLOPS = 2 * SAMPLES * (64 + 16) * CHANNELS * COLUMNS


def load_x_tile(nc, pools, x, positions, first):
    passes = QUANT_WIDTH // (PACK * SAMPLES * positions)
    raw = pools["x_raw"].tile([P, passes, SAMPLES, PACK * positions], BF16, name="x_raw")
    for i in range(passes):
        rows = slice((first + i) * K_PASS, (first + i + 1) * K_PASS)
        nc.sync.dma_start(
            out=raw[:, i], in_=x[:, rows].rearrange("n (q t) h w -> q n (t h w)", t=PACK)
        )
    return raw


def regroup_x_tile(nc, pools, raw, positions, copy):
    grouped = pools["x_grouped"].tile([P, QUANT_WIDTH // (PACK * positions), positions, PACK], BF16,
                                      name="x_grouped", align_bytes=64)
    copy(
        out=grouped[:].rearrange("q a (c i) t -> q a c t i", i=4),
        in_=raw[:].rearrange("q l n (t c i) -> q (l n) c t i", t=PACK, i=4),
    )
    return grouped


def quantise_x_tile(nc, grouped, codes, scales, first, positions):
    these = slice(first, first + QUANT_WIDTH // (PACK * SAMPLES * positions))
    nc.vector.quantize_mx(
        out=codes[:, these, :].rearrange("q c m -> q (c m)").bitcast(FP8X4),
        scales=scales[:, these, :].rearrange("q c m -> q (c m)"),
        in_=grouped[:].rearrange("q a f t -> q (a f t)"),
    )


def group_statistics(pools):
    chunk_max = pools["stats"].tile([P, LANES, CHUNKS], F32, name="chunk_max")
    shift = pools["stats"].tile([P, LANES, CHUNKS], F32, name="shift")
    sums = pools["stats"].tile([P, LANES, CHUNKS, CHUNK_PASSES], F32, name="sums")
    return chunk_max, shift, sums


def load_w_chunk(nc, pools, w, group, chunk):
    columns = slice(group * GROUP_COLUMNS, (group + 1) * GROUP_COLUMNS)
    w_chunk = pools["w"].tile([P, CHUNK_PASSES, PACK, GROUP_COLUMNS], BF16, name="w_chunk")
    for l in range(CHUNK_PASSES):
        first_row = (chunk * CHUNK_PASSES + l) * K_PASS
        nc.sync.dma_start(
            out=w_chunk[:, l],
            in_=w[first_row : first_row + K_PASS, columns].rearrange("(q t) o -> q t o", t=PACK),
        )
    return w_chunk


def halve_rows(nc, pools, w_chunk, best, rows):
    half = rows * GROUP_COLUMNS
    if best is None:
        best = pools["best"].tile([P, half], BF16, name="best")
        nc.vector.tensor_tensor(
            out=best[:],
            in0=w_chunk[:, 0:2].rearrange("q l t o -> q (l t o)"),
            in1=w_chunk[:, 2:4].rearrange("q l t o -> q (l t o)"),
            op=ALU.max,
        )
    else:
        nc.vector.tensor_tensor(
            out=best[:, 0:half], in0=best[:, 0:half], in1=best[:, half : 2 * half], op=ALU.max
        )
    return best


def chunk_maxima(nc, pools, ident, best, statistics, chunk):
    chunk_max = statistics[0]
    best_t = pools["psum_small"].tile([P, P], F32, name="best_t", tag="small")
    nc.tensor.transpose(best_t[:], best[:, 0:GROUP_COLUMNS].bitcast(F32), ident[:])
    nc.vector.tensor_reduce(
        out=chunk_max[:, :, chunk],
        in_=best_t[:].bitcast(BF16).rearrange("i (q e) -> i e q", e=LANES),
        axis=AXIS_X,
        op=ALU.max,
    )


def chunk_shift(nc, statistics, chunk):
    chunk_max, shift = statistics[0], statistics[1]
    nc.scalar.activation(
        out=shift[:, :, chunk], in_=chunk_max[:, :, chunk], func=ACT.Copy, scale=-GRAD_BOOST
    )


def transpose_pass(nc, pools, ident, w_chunk, l):
    w_words = w_chunk[:].bitcast(F32)
    w_t = pools["psum_w"].tile([P, PACK, P], F32, name="w_t")
    for t in range(PACK):
        nc.tensor.transpose(w_t[:, t, :], w_words[:, l, t, :], ident[:])
    return w_t


def exponentials(nc, w_t, e_lanes, statistics, chunk, l):
    shift, sums = statistics[1], statistics[2]
    by_lane = w_t[:].bitcast(BF16).rearrange("i (u k) (q e) -> i e u q k", k=2, e=LANES)
    for lane in range(LANES):
        nc.scalar.activation(
            out=e_lanes[lane][:, l * K_PASS : (l + 1) * K_PASS].rearrange(
                "i (u q k) -> i u q k", u=2, k=2
            ),
            in_=by_lane[:, lane],
            func=ACT.Exp,
            bias=shift[:, lane, chunk : chunk + 1],
            scale=GRAD_BOOST,
            accum_out=sums[:, lane, chunk, l : l + 1],
        )


def below_column_max(nc, pools, statistics):
    chunk_max = statistics[0]
    shape = [P, LANES, CHUNKS]
    col_max = pools["stats"].tile([P, LANES], F32, name="col_max")
    nc.vector.tensor_reduce(out=col_max[:], in_=chunk_max[:], axis=AXIS_X, op=ALU.max)
    below = pools["stats"].tile(shape, F32, name="below")
    nc.vector.tensor_tensor(
        out=below[:], in0=chunk_max[:], in1=col_max[:].unsqueeze(2).to_broadcast(shape), op=ALU.subtract
    )
    return below


def chunk_rescale(nc, pools, below):
    rescale = pools["stats"].tile([P, LANES, CHUNKS], F32, name="rescale")
    nc.scalar.activation(out=rescale[:], in_=below[:], func=ACT.Exp, scale=GRAD_BOOST)
    return rescale


def column_gain(nc, pools, statistics, rescale):
    sums = statistics[2]
    shape = [P, LANES, CHUNKS]
    chunk_sum = pools["stats"].tile(shape, F32, name="chunk_sum")
    nc.vector.tensor_reduce(out=chunk_sum[:], in_=sums[:], axis=AXIS_X, op=ALU.add)
    nc.vector.tensor_tensor(out=chunk_sum[:], in0=chunk_sum[:], in1=rescale[:], op=ALU.mult)
    col_sum = pools["stats"].tile([P, LANES], F32, name="col_sum")
    nc.vector.tensor_reduce(out=col_sum[:], in_=chunk_sum[:], axis=AXIS_X, op=ALU.add)
    nc.vector.reciprocal(out=col_sum[:], in_=col_sum[:])
    gain = pools["stats"].tile(shape, F32, name="gain")
    nc.vector.tensor_tensor(
        out=gain[:], in0=rescale[:], in1=col_sum[:].unsqueeze(2).to_broadcast(shape), op=ALU.mult
    )
    return gain


def normalise(nc, pools, e_lane, gain_column, on_scalar):
    sm_t = pools["sm_t"].tile([P, CHUNK_CHANNELS], BF16, name="sm_t")
    cut = CHUNK_CHANNELS - on_scalar
    nc.vector.tensor_scalar(
        out=sm_t[:, 0:cut], in0=e_lane[:, 0:cut], scalar1=gain_column, scalar2=None, op0=ALU.mult
    )
    if on_scalar:
        nc.scalar.activation(out=sm_t[:, cut:], in_=e_lane[:, cut:], func=ACT.Copy, scale=gain_column)
    return sm_t


def transpose_back(nc, pools, ident, sm_t):
    sm_words = sm_t[:].bitcast(F32)
    grouped = pools["sm_grouped"].tile([P, CHUNK_PASSES, P, PACK], BF16, name="sm_grouped", align_bytes=64)
    grouped_words = grouped[:].bitcast(F32)
    for pair in range(CHUNK_PASSES // 2):
        back = pools["psum_back"].tile([P, 4, P], F32, name="back")
        for r in range(4):
            run = (4 * pair + r) * P
            nc.tensor.transpose(back[:, r, :], sm_words[:, run : run + P], ident[:])
        nc.scalar.copy(
            out=grouped_words[:, 2 * pair : 2 * pair + 2],
            in_=back[:].rearrange("q (l u) i -> q l i u", u=2),
        )
    return grouped


def quantise_sm(nc, pools, grouped):
    sm_codes = pools["codes"].tile([P, CHUNK_PASSES * P], U32, name="sm_codes", align_bytes=64)
    sm_scales = pools["codes"].tile([P, CHUNK_PASSES * P], U8, name="sm_scales", align_bytes=64)
    nc.vector.quantize_mx(
        out=sm_codes[:].bitcast(FP8X4),
        scales=sm_scales[:],
        in_=grouped[:].rearrange("q l i t -> q (l i t)"),
    )
    return sm_codes, sm_scales


def multiply(nc, proj_lane, sm_codes, sm_scales, x_codes, x_scales, chunk):
    for l in range(CHUNK_PASSES):
        c = chunk * CHUNK_PASSES + l
        nc.tensor.matmul_mx(
            out=proj_lane,
            lhsT=sm_codes[:, l * P : (l + 1) * P].bitcast(FP8X4),
            lhsT_scale=sm_scales[:, l * P : (l + 1) * P],
            rhs=x_codes[:, c, :].bitcast(FP8X4),
            rhs_scale=x_scales[:, c, :],
            start=(c == 0),
            stop=(c == PASSES - 1),
        )


def square(nc, pools, proj, width):
    squares = []
    for lane in range(LANES):
        squares.append(pools["row"].tile([P, COLUMNS], F32, name="squares%d" % lane, tag="row"))
        nc.scalar.activation(out=squares[lane][:, 0:width], in_=proj[lane][:, 0:width], func=ACT.Square)
    return squares


def sum_positions(nc, squares, width, q_t, first_slot, first_col):
    for lane in range(LANES):
        nc.vector.tensor_reduce(
            out=q_t[:, first_slot + lane, first_col : first_col + SAMPLES],
            in_=squares[lane][:, 0:width].rearrange("i (n f) -> i n f", n=SAMPLES),
            axis=AXIS_X,
            op=ALU.add,
        )


def normalise_rows(nc, pools, ident, q_t, out):
    rows = 2 * SAMPLES
    q_rows = pools["psum_small"].tile([P, 2 * GROUPS, P], F32, name="q_rows", tag="small")
    for slot in range(2 * GROUPS):
        nc.tensor.transpose(q_rows[:, slot, :], q_t[:, slot, :], ident[:])
    stats = pools["stats"]
    moments = stats.tile([P, 6], F32, name="moments")
    nc.vector.bn_stats(out=moments[0:rows], in_=q_rows[0:rows].rearrange("r s i -> r (s i)"))
    mean_var = stats.tile([P, 2], F32, name="mean_var")
    nc.vector.bn_aggr(out=mean_var[0:rows], in_=moments[0:rows])
    std = stats.tile([P, 1], F32, name="std")
    nc.scalar.activation(
        out=std[0:rows], in_=mean_var[0:rows, 1:2], func=ACT.Sqrt, scale=COLUMNS / (COLUMNS - 1.0)
    )
    inverse = stats.tile([P, 1], F32, name="inverse")
    nc.vector.tensor_scalar(
        out=inverse[0:rows], in0=std[0:rows], scalar1=EPS, scalar2=None, op0=ALU.add
    )
    nc.vector.reciprocal(out=inverse[0:rows], in_=inverse[0:rows])
    result = pools["row"].tile([P, COLUMNS], F32, name="result", tag="row")
    nc.vector.tensor_scalar(
        out=result[0:rows].rearrange("r (g i e) -> r g i e", g=GROUPS, e=LANES),
        in0=q_rows[0:rows].rearrange("r (g e) i -> r g i e", e=LANES),
        scalar1=mean_var[0:rows, 0:1],
        scalar2=inverse[0:rows, 0:1],
        op0=ALU.subtract,
        op1=ALU.mult,
    )
    for s in range(2):
        nc.sync.dma_start(
            out=out[:, s * COLUMNS : (s + 1) * COLUMNS], in_=result[s * SAMPLES : (s + 1) * SAMPLES]
        )


def tile_texture_encoder_pa_k_kernel(tc, x3, x4, w1_3, w1_4, out):
    nc = tc.nc
    with ExitStack() as ctx:
        sbuf_pools = {
            "const": 1,
            "x_keep": 1,
            "x_raw": 3,
            "x_grouped": 3,
            "w": W_AHEAD + 1,
            "best": 2,
            "e": LANES * CHUNKS + LANES,
            "sm_t": LANES,
            "sm_grouped": LANES,
            "codes": 2 * LANES,
            "row": 3,
            "stats": 2,
        }
        psum_pools = {"psum_w": 3, "psum_back": 2, "psum_proj": LANES, "psum_small": 1}
        pools = {}
        for name, bufs in sbuf_pools.items():
            pools[name] = ctx.enter_context(tc.tile_pool(name=name, bufs=bufs))
        for name, bufs in psum_pools.items():
            pools[name] = ctx.enter_context(tc.psum_pool(name=name, bufs=bufs))

        ctx.enter_context(tc.manual_schedule(engines={mybir.EngineType.SP}))

        ident = pools["const"].tile([P, P], F32, name="ident")
        make_identity(nc, ident[:])
        q_t = pools["const"].tile([P, 2 * GROUPS, P], F32, name="q_t")
        nc.vector.memset(q_t[:], 0.0)
        warm = pools["const"].tile([P, 1], F32, name="warm")
        nc.vector.memset(warm[:], 0.0)
        nc.scalar.activation(out=warm[:], in_=warm[:], func=ACT.Exp)

        x4_codes = pools["x_keep"].tile([P, PASSES, SAMPLES * 16], U32, name="x4_codes", align_bytes=64)
        x4_scales = pools["x_keep"].tile([P, PASSES, SAMPLES * 16], U8, name="x4_scales", align_bytes=64)
        x3_codes = pools["x_keep"].tile([P, PASSES, SAMPLES * 64], U32, name="x3_codes", align_bytes=64)
        x3_scales = pools["x_keep"].tile([P, PASSES, SAMPLES * 64], U8, name="x3_scales", align_bytes=64)

        jobs = []
        for group in range(GROUPS):
            jobs.append((w1_4, group, x4_codes, x4_scales, 16, SAMPLES))
        for group in range(GROUPS):
            jobs.append((w1_3, group, x3_codes, x3_scales, 64, 0))
        steps = len(jobs) * CHUNKS

        x_tiles = {}
        for c in range(PASSES):
            x_tiles[c - 1 if c else -2] = [(x3, 64, x3_codes, x3_scales, c)]
        for i in range(4):
            x_tiles[X4_FIRST_STEP + i].append((x4, 16, x4_codes, x4_scales, 4 * i))

        w_chunks, bests, w_ts, statistics, belows, rescales, gains = {}, {}, {}, {}, {}, {}, {}
        e_tiles, sm_ts, sm_groups, quantised, projs, squares, x_raws, x_groups = {}, {}, {}, {}, {}, {}, {}, {}

        first_tile = x_tiles[-2][0]
        x_raws[-2] = [load_x_tile(nc, pools, first_tile[0], first_tile[1], first_tile[4])]
        for s in range(-W_AHEAD, steps + STAGE3_LAG + 3):
            mid, done = s - STAGE2_LAG, s - STAGE3_LAG
            has_new, has_mid, has_done = 0 <= s < steps, 0 <= mid < steps, 0 <= done < steps
            has_next, has_tree = 0 <= s + 1 < steps, 0 <= s + 2 < steps

            if s + W_AHEAD < steps:
                w, group = jobs[(s + W_AHEAD) // CHUNKS][0:2]
                w_chunks[s + W_AHEAD] = load_w_chunk(nc, pools, w, group, (s + W_AHEAD) % CHUNKS)

            if has_tree:
                bests[s + 2] = halve_rows(nc, pools, w_chunks[s + 2], None, 8)
            if has_next:
                job, chunk = (s + 1) // CHUNKS, (s + 1) % CHUNKS
                if chunk == 0:
                    statistics[job] = group_statistics(pools)
                chunk_maxima(nc, pools, ident, bests[s + 1], statistics[job], chunk)
            if has_done:
                quantised[done] = [quantise_sm(nc, pools, sm_groups[done][0])]
            if has_tree:
                halve_rows(nc, pools, w_chunks[s + 2], bests[s + 2], 4)
            if has_next:
                job, chunk = (s + 1) // CHUNKS, (s + 1) % CHUNKS
                chunk_shift(nc, statistics[job], chunk)
                if chunk == CHUNKS - 1:
                    belows[job] = below_column_max(nc, pools, statistics[job])
            if has_mid:
                job, chunk = mid // CHUNKS, mid % CHUNKS
                if chunk == 0:
                    gains[job] = column_gain(nc, pools, statistics[job], rescales[job])
                sm_ts[mid] = [normalise(nc, pools, e_tiles[mid][0], gains[job][:, 0, chunk : chunk + 1], 0)]
            if has_tree:
                halve_rows(nc, pools, w_chunks[s + 2], bests[s + 2], 2)
            if has_mid:
                sm_ts[mid].append(normalise(nc, pools, e_tiles[mid][1], gains[job][:, 1, chunk : chunk + 1], SCALAR_SHARE if mid < SHARED_STEPS else 0))
            if has_tree:
                halve_rows(nc, pools, w_chunks[s + 2], bests[s + 2], 1)
            if has_done:
                quantised[done].append(quantise_sm(nc, pools, sm_groups[done][1]))
            for grouped, tile in zip(x_groups.get(s - 1, []), x_tiles.get(s - 1, [])):
                quantise_x_tile(nc, grouped, tile[2], tile[3], tile[4], tile[1])
            x_groups[s] = [
                regroup_x_tile(nc, pools, raw, tile[1], nc.vector.tensor_copy)
                for raw, tile in zip(x_raws.get(s, []), x_tiles.get(s, []))
            ]
            if 0 <= done - 2 < steps and (done - 2) % CHUNKS == CHUNKS - 1:
                ready = (done - 2) // CHUNKS
                group, positions, first_col = jobs[ready][1], jobs[ready][4], jobs[ready][5]
                sum_positions(nc, squares[ready], SAMPLES * positions, q_t, LANES * group, first_col)
            if s + 1 not in x_raws:
                x_raws[s + 1] = [
                    load_x_tile(nc, pools, tile[0], tile[1], tile[4]) for tile in x_tiles.get(s + 1, [])
                ]

            if has_new:
                job, chunk = s // CHUNKS, s % CHUNKS
                e_tiles[s] = [
                    pools["e"].tile([P, CHUNK_CHANNELS], F32, name="e_lane%d" % lane, tag="e_tile")
                    for lane in range(LANES)
                ]
                for l in range(PASSES_AHEAD):
                    exponentials(nc, w_ts[(s, l)], e_tiles[s], statistics[job], chunk, l)
            if has_mid:
                sm_groups[mid] = [transpose_back(nc, pools, ident, sm_ts[mid][0])]
            if 0 <= done - 1 < steps and (done - 1) % CHUNKS == CHUNKS - 1:
                ready = (done - 1) // CHUNKS
                positions = jobs[ready][4]
                squares[ready] = square(nc, pools, projs[ready], SAMPLES * positions)
            if has_new:
                for l in range(PASSES_AHEAD, CHUNK_PASSES):
                    w_ts[(s, l)] = transpose_pass(nc, pools, ident, w_chunks[s], l)
                    exponentials(nc, w_ts[(s, l)], e_tiles[s], statistics[job], chunk, l)
            if has_mid:
                sm_groups[mid].append(transpose_back(nc, pools, ident, sm_ts[mid][1]))
            if has_next and (s + 1) % CHUNKS == CHUNKS - 1:
                rescales[(s + 1) // CHUNKS] = chunk_rescale(nc, pools, belows[(s + 1) // CHUNKS])
            if s == steps - 1:
                nc.scalar.activation(out=warm[:], in_=statistics[job][2][:, LANES - 1, chunk, CHUNK_PASSES - 1 :], func=ACT.Sqrt)

            if has_done:
                job, chunk = done // CHUNKS, done % CHUNKS
                x_codes, x_scales, positions = jobs[job][2:5]
                if chunk == 0:
                    projs[job] = [
                        pools["psum_proj"].tile([P, COLUMNS], F32, name="proj%d" % lane, tag="proj")
                        for lane in range(LANES)
                    ]
                for lane in range(LANES):
                    sm_codes, sm_scales = quantised[done][lane]
                    multiply(
                        nc, projs[job][lane][:, 0 : SAMPLES * positions], sm_codes, sm_scales,
                        x_codes, x_scales, chunk,
                    )
            if has_next:
                for l in range(PASSES_AHEAD):
                    w_ts[(s + 1, l)] = transpose_pass(nc, pools, ident, w_chunks[s + 1], l)
        normalise_rows(nc, pools, ident, q_t, out)
